import numpy as np
import ml_dtypes


def mxq(x, axis, fmt="e4m3"):
    dtype, down = {"e4m3": (ml_dtypes.float8_e4m3fn, 7), "e5m2": (ml_dtypes.float8_e5m2, 14)}[fmt]
    v = np.moveaxis(np.asarray(x, np.float32).astype(ml_dtypes.bfloat16).astype(np.float64), axis, -1)
    blocks = v.reshape(v.shape[:-1] + (-1, 32))
    amax = np.abs(blocks).max(-1, keepdims=True)
    byte = np.maximum(np.where(amax > 0, np.frexp(amax)[1] - 1 + 127, 0) - down, 1)
    scale = np.exp2(byte - 127.0)
    codes = (blocks / scale).astype(np.float32).astype(dtype).astype(np.float64)
    return np.moveaxis((codes * scale).reshape(v.shape), -1, axis)


WIDE = False


def mx_kscale(k):
    if not WIDE:
        return np.ones(k)
    levels = np.array([10, -10, 5, -5, 0])
    a = np.random.permutation(np.resize(levels, k // 512 * 4)).reshape(k // 512, 4)
    idx = np.arange(k)
    return np.exp2(a[idx // 512, idx % 128 // 32])


BF16 = ml_dtypes.bfloat16


def bf(x):
    return np.asarray(x, np.float32).astype(BF16)


def f64(x):
    return np.asarray(x).astype(np.float64)


B, S, D, C, M, H = 4, 256, 1024, 16, 512, 4
LN_EPS = 1e-5


def sigmoid(v):
    return 1.0 / (1.0 + np.exp(-v))


def setup_inputs():
    s = mx_kscale(M)
    t = mx_kscale(M)
    u = mx_kscale(M)
    g = np.concatenate([np.ones(D), u])
    return {
        "x": bf(np.random.standard_normal((B, S, D))),
        "query": bf(np.random.standard_normal((B, S, M)) * u),
        "ctx": bf(np.random.standard_normal((B, S, M)) * 0.5 * s),
        "attn_out_w": bf(np.random.standard_normal((M, M)) * 2.0 / np.sqrt(M) * t[:, None] / s[None, :]),
        "attn_out_b": bf(np.random.standard_normal(M) * 0.3 * t),
        "op_w": bf(np.random.standard_normal((D, M)) / np.sqrt(M) / t[None, :]),
        "op_b": bf(np.random.standard_normal(D) * 0.3 + 0.3),
        "gate_w": bf(np.random.standard_normal((D, D + M)) / np.sqrt(D + M) / g[None, :]),
        "gate_b": bf(np.random.standard_normal(D) * 0.5),
        "ln_g": bf(1.0 + 0.1 * np.random.standard_normal(D)),
        "ln_b": bf(0.1 * np.random.standard_normal(D)),
    }


def reference(x, query, ctx, attn_out_w, attn_out_b, op_w, op_b, gate_w, gate_b, ln_g, ln_b):
    x = f64(x)
    r = (mxq(f64(ctx), 2, "e4m3") @ mxq(f64(attn_out_w), 1, "e4m3").T) + f64(attn_out_b)
    retrieved = (mxq(r, 2, "e4m3") @ mxq(f64(op_w), 1, "e4m3").T) + f64(op_b)
    gate_in = np.concatenate([x, f64(query)], axis=-1)
    gate = sigmoid((mxq(gate_in, 2, "e4m3") @ mxq(f64(gate_w), 1, "e4m3").T) + f64(gate_b))
    y = gate * x + (1.0 - gate) * retrieved
    mu = y.mean(axis=-1, keepdims=True)
    var = y.var(axis=-1, keepdims=True)
    return (y - mu) / np.sqrt(var + LN_EPS) * f64(ln_g) + f64(ln_b)

@@ -1,0 +1,278 @@
+from contextlib import ExitStack
+
+import concourse.mybir as mybir
+from concourse.masks import make_identity
+
+F32 = mybir.dt.float32
+BF16 = mybir.dt.bfloat16
+U32 = mybir.dt.uint32
+U8 = mybir.dt.uint8
+FP8X4 = mybir.dt.float8_e4m3fn_x4
+ACT = mybir.ActivationFunctionType
+ALU = mybir.AluOpType
+
+P = 128
+T = 1024
+D = 1024
+M = 512
+HALF = 512
+LN_EPS = 1e-5
+
+FLOPS = 2 * T * (M * M + M * D + (D + M) * D)
+
+
+def tile_rotelearningmemory_pa_kernel(
+    tc, x, query, ctx, attn_out_w, attn_out_b, op_w, op_b, gate_w, gate_b, ln_g, ln_b, out
+):
+    nc = tc.nc
+
+    def pairs(a):
+        return a.rearrange("(i q e) k -> q i (e k)", q=P, e=2)
+
+    x_d = pairs(x.flatten_outer_dims())
+    q_d = pairs(query.flatten_outer_dims())
+    c_d = pairs(ctx.flatten_outer_dims())
+    aw_d = pairs(attn_out_w)
+    ow_d = pairs(op_w)
+    gw_d = pairs(gate_w)
+    out_d = out.flatten_outer_dims().rearrange("(i q e) d -> q i e d", q=P, e=2)
+
+    with ExitStack() as stack:
+        keep = stack.enter_context(tc.tile_pool(name="keep", bufs=1))
+        actraw = stack.enter_context(tc.tile_pool(name="actraw", bufs=4))
+        wraw = stack.enter_context(tc.tile_pool(name="wraw", bufs=2))
+        grp = stack.enter_context(tc.tile_pool(name="grp", bufs=3))
+        grpw = stack.enter_context(tc.tile_pool(name="grpw", bufs=2))
+        rpool = stack.enter_context(tc.tile_pool(name="rpool", bufs=1))
+        mpool = stack.enter_context(tc.tile_pool(name="mpool", bufs=2))
+        work = stack.enter_context(tc.tile_pool(name="work", bufs=2))
+        small = stack.enter_context(tc.tile_pool(name="small", bufs=4))
+        psum = stack.enter_context(tc.psum_pool(name="psum", bufs=2))
+
+        ident_f = keep.tile([P, P], F32)
+        make_identity(nc, ident_f[:])
+        ident_b = keep.tile([P, P], BF16)
+        make_identity(nc, ident_b[:])
+        mhalf = keep.tile([P, 1], F32)
+        nc.gpsimd.memset(mhalf[:], -0.5)
+        warm_in = keep.tile([P, 1], F32)
+        nc.vector.memset(warm_in[:], 0.0)
+        warm_out = keep.tile([P, 1], F32)
+        nc.scalar.activation(out=warm_out[:], in_=warm_in[:], func=ACT.Sigmoid)
+        vec = keep.tile([P, 256], BF16)
+        nc.vector.memset(vec[:].bitcast(F32), 0.0)
+
+        nc.scalar.dma_start(out=vec[8:10, :], in_=attn_out_b.rearrange("(r c) -> r c", c=256))
+        nc.scalar.dma_start(out=vec[0:4, :], in_=gate_b.rearrange("(r c) -> r c", c=256))
+        nc.scalar.dma_start(out=vec[4:8, :], in_=op_b.rearrange("(r c) -> r c", c=256))
+
+        x_raw = keep.tile([P, 4, 2 * D], BF16)
+        c_raw = []
+        q_raw = []
+        gw_raw = []
+        ow_raw = []
+
+        def load_act(src, th, nm):
+            t = actraw.tile([P, 2, 2 * M], BF16, name=nm, tag="act")
+            nc.sync.dma_start(out=t[:], in_=src[:, 2 * th : 2 * th + 2, :])
+            return t
+
+        c_raw.append(load_act(c_d, 0, "c_raw0"))
+        aw_raw = load_act(aw_d, 0, "aw_raw")
+        nc.sync.dma_start(out=x_raw[:, 0:2, :], in_=x_d[:, 0:2, :])
+        q_raw.append(load_act(q_d, 0, "q_raw0"))
+        for i in range(4):
+            g_t = wraw.tile([P, 2 * (D + M)], BF16, name="gw_raw%d" % i, tag="gwraw")
+            nc.sync.dma_start(out=g_t[:], in_=gw_d[:, i, :])
+            gw_raw.append(g_t)
+            o_t = wraw.tile([P, 2 * M], BF16, name="ow_raw%d" % i, tag="owraw")
+            nc.sync.dma_start(out=o_t[:], in_=ow_d[:, i, :])
+            ow_raw.append(o_t)
+        c_raw.append(load_act(c_d, 1, "c_raw1"))
+        nc.sync.dma_start(out=x_raw[:, 2:4, :], in_=x_d[:, 2:4, :])
+        q_raw.append(load_act(q_d, 1, "q_raw1"))
+        lg_bc = keep.tile([P, D], BF16)
+        nc.scalar.dma_start(out=lg_bc[:], in_=ln_g.partition_broadcast(P))
+        lb_bc = keep.tile([P, D], BF16)
+        nc.scalar.dma_start(out=lb_bc[:], in_=ln_b.partition_broadcast(P))
+
+        cc = keep.tile([P, T], U32, align_bytes=64)
+        cs = keep.tile([P, T], U8, align_bytes=64)
+        wa = keep.tile([P, M], U32, align_bytes=64)
+        was = keep.tile([P, M], U8, align_bytes=64)
+        gc = keep.tile([P, 2 * 3 * HALF], U32, align_bytes=64)
+        gs = keep.tile([P, 2 * 3 * HALF], U8, align_bytes=64)
+        wc = keep.tile([P, 4 * 4 * 256], U32, align_bytes=64)
+        ws = keep.tile([P, 4 * 4 * 256], U8, align_bytes=64)
+        rc = keep.tile([P, T], U32, align_bytes=64)
+        rs = keep.tile([P, T], U8, align_bytes=64)
+        gx = keep.tile([P, 2 * 2 * HALF * 4], BF16, align_bytes=64)
+
+        def words(t3):
+            return t3[:].rearrange("p i k -> p (i k)").bitcast(F32)
+
+        def bank(src_words, base, row_words, dst_bf16, eng):
+            tp = psum.tile([P, 2, 256], F32, tag="tp")
+            for u in range(2):
+                for e in range(2):
+                    o = base + e * row_words + u * P
+                    nc.tensor.transpose(tp[:, u, e * P : (e + 1) * P], src_words[:, o : o + P], ident_f[:])
+            dst = dst_bf16.bitcast(F32).rearrange("p (r u) -> p r u", u=2)
+            src = tp[:].rearrange("p u r -> p r u")
+            if eng == "v":
+                nc.vector.tensor_copy(out=dst, in_=src)
+            else:
+                nc.scalar.copy(out=dst, in_=src)
+
+        def quant(src, codes, scales):
+            nc.vector.quantize_mx(out=codes.bitcast(FP8X4), scales=scales, in_=src)
+
+        def mx(acc, lw, lsc, rw, rsc, start, stop):
+            nc.tensor.matmul_mx(
+                out=acc, lhsT=lw.bitcast(FP8X4), lhsT_scale=lsc, rhs=rw.bitcast(FP8X4), rhs_scale=rsc,
+                start=start, stop=stop,
+            )
+
+        vt = psum.tile([P, 2, 256], F32, tag="tp")
+        nc.tensor.transpose(vt[:, 0, 0:P], vec[:].bitcast(F32), ident_f[:])
+        vt_b = vt[:, 0, 0:16].bitcast(BF16)
+        ngb = keep.tile([P, 8], F32)
+        nc.vector.tensor_scalar_mul(out=ngb[:], in0=vt_b[:, 0:8], scalar1=-1.0)
+        ob = keep.tile([P, 8], F32)
+        nc.vector.tensor_copy(out=ob[:], in_=vt_b[:, 8:16])
+        ab = keep.tile([P, 4], F32)
+        nc.vector.tensor_copy(out=ab[:], in_=vt_b[:, 16:20])
+
+        def front_small(raw_t, codes, scales, engs):
+            g = grp.tile([P, 4 * HALF], BF16, tag="ga", align_bytes=64)
+            w = words(raw_t)
+            for il in range(2):
+                bank(w, il * M, M // 2, g[:, il * 1024 : (il + 1) * 1024], engs[il])
+            quant(g[:], codes, scales)
+
+        def front_x(th, engs):
+            w = words(x_raw)
+            n = 0
+            for g in range(2):
+                for il in range(2):
+                    a = ((th * 2 + g) * HALF + il * 256) * 4
+                    bank(w, (2 * th + il) * D + g * 256, D // 2, gx[:, a : a + 1024], engs[n])
+                    n += 1
+            quant(
+                gx[:, th * 4096 : (th + 1) * 4096],
+                gc[:, th * 1536 : th * 1536 + 1024],
+                gs[:, th * 1536 : th * 1536 + 1024],
+            )
+
+        def front_w(i, engs):
+            g = grpw.tile([P, 4 * 4 * 256], BF16, tag="gw", align_bytes=64)
+            gww = gw_raw[i][:].bitcast(F32)
+            for s in range(3):
+                bank(gww, s * 256, (D + M) // 2, g[:, s * 1024 : (s + 1) * 1024], engs[s])
+            bank(ow_raw[i][:].bitcast(F32), 0, M // 2, g[:, 3072:4096], engs[3])
+            quant(g[:], wc[:, i * 1024 : (i + 1) * 1024], ws[:, i * 1024 : (i + 1) * 1024])
+
+        def mm1(th):
+            r_t = rpool.tile([P, 4, HALF], BF16, tag="rT")
+            for t in range(4):
+                p1 = psum.tile([P, HALF], F32, name="p1_%d_%d" % (th, t), tag=("p3" if t % 2 == 0 else "p2"))
+                mx(
+                    p1[:], wa[:, t * P : (t + 1) * P], was[:, t * P : (t + 1) * P],
+                    cc[:, th * HALF : (th + 1) * HALF], cs[:, th * HALF : (th + 1) * HALF], True, True,
+                )
+                nc.scalar.activation(out=r_t[:, t, :], in_=p1[:], func=ACT.Identity, bias=ab[:, t : t + 1], scale=1.0)
+            g_r = rpool.tile([P, HALF, 4], BF16, tag="gr", align_bytes=64)
+            nc.vector.tensor_copy(out=g_r[:], in_=r_t[:].rearrange("p t c -> p c t"))
+            quant(
+                g_r[:].rearrange("p c t -> p (c t)"),
+                rc[:, th * HALF : (th + 1) * HALF], rs[:, th * HALF : (th + 1) * HALF],
+            )
+
+        gx5 = gx[:].rearrange("p (h g c t) -> p h g c t", h=2, g=2, t=4)
+
+        def gating(th, i, e, m_t):
+            d = 2 * i + e
+            p3 = psum.tile([P, HALF], F32, tag="p3")
+            for s in range(3):
+                a = (i * 4 + s) * 256 + e * P
+                b = (th * 3 + s) * HALF
+                mx(p3[:], wc[:, a : a + P], ws[:, a : a + P], gc[:, b : b + HALF], gs[:, b : b + HALF], s == 0, s == 2)
+            p2 = psum.tile([P, HALF], F32, tag="p2")
+            a = (i * 4 + 3) * 256 + e * P
+            mx(
+                p2[:], wc[:, a : a + P], ws[:, a : a + P],
+                rc[:, th * HALF : (th + 1) * HALF], rs[:, th * HALF : (th + 1) * HALF], True, True,
+            )
+            h_t = work.tile([P, HALF], F32, tag="h")
+            nc.scalar.activation(out=h_t[:], in_=p3[:], func=ACT.Sigmoid, bias=ngb[:, d : d + 1], scale=-1.0)
+            e_t = work.tile([P, HALF], F32, tag="e")
+            nc.vector.scalar_tensor_tensor(
+                out=e_t[:], in0=p2[:], scalar=ob[:, d : d + 1], in1=gx5[:, th, i // 2, :, 2 * (i % 2) + e],
+                op0=ALU.add, op1=ALU.subtract,
+            )
+            nc.vector.tensor_tensor(out=m_t[:, d, :], in0=h_t[:], in1=e_t[:], op=ALU.mult)
+
+        def layernorm(th, j, m_t):
+            i_tok = 2 * th + j // 2
+            e_tok = j % 2
+            y_t = work.tile([P, D], F32, tag="y")
+            s1 = small.tile([P, 2], F32, tag="s1")
+            for g in range(2):
+                yp = psum.tile([P, 2, 256], F32, tag="y")
+                nc.tensor.matmul(
+                    out=yp[:], lhsT=ident_b[:],
+                    rhs=x_raw[:, i_tok, e_tok * D + g * 512 : e_tok * D + (g + 1) * 512].rearrange("p (a e) -> p e a", e=2),
+                    start=True, stop=False,
+                )
+                for e in range(2):
+                    for u in range(2):
+                        nc.tensor.matmul(
+                            out=yp[:, e, u * P : (u + 1) * P], lhsT=m_t[:, 2 * (2 * g + u) + e, j * P : (j + 1) * P],
+                            rhs=ident_f[:], is_transpose=True, start=False, stop=(e == 1 and u == 1),
+                        )
+                nc.scalar.activation(
+                    out=y_t[:, g * 512 : (g + 1) * 512].rearrange("p (a e) -> p a e", e=2),
+                    in_=yp[:].rearrange("p e a -> p a e"), func=ACT.Identity, accum_out=s1[:, g : g + 1],
+                )
+            nmean = small.tile([P, 1], F32, tag="nmean")
+            nc.gpsimd.tensor_scalar(
+                out=nmean[:], in0=s1[:, 0:1], scalar1=s1[:, 1:2], scalar2=-1.0 / D, op0=ALU.add, op1=ALU.mult
+            )
+            junk = work.tile([P, D], BF16, tag="junk")
+            s2 = small.tile([P, 1], F32, tag="s2")
+            nc.scalar.activation(out=junk[:], in_=y_t[:], func=ACT.Square, bias=nmean[:], scale=1.0, accum_out=s2[:])
+            w_t = work.tile([P, D], F32, tag="w")
+            nc.vector.scalar_tensor_tensor(
+                out=w_t[:], in0=y_t[:], scalar=nmean[:], in1=lg_bc[:], op0=ALU.add, op1=ALU.mult
+            )
+            ve = small.tile([P, 1], F32, tag="ve")
+            nc.gpsimd.tensor_scalar(out=ve[:], in0=s2[:], scalar1=1.0 / D, scalar2=LN_EPS, op0=ALU.mult, op1=ALU.add)
+            rstd = small.tile([P, 1], F32, tag="rstd")
+            nc.gpsimd.tensor_tensor(out=rstd[:], in0=ve[:], in1=mhalf[:], op=ALU.pow)
+            o_t = work.tile([P, D], F32, tag="o")
+            nc.vector.scalar_tensor_tensor(
+                out=o_t[:], in0=w_t[:], scalar=rstd[:], in1=lb_bc[:], op0=ALU.mult, op1=ALU.add
+            )
+            nc.sync.dma_start(out=out_d[:, i_tok, e_tok, :], in_=o_t[:])
+
+        front_small(c_raw[0], cc[:, 0:HALF], cs[:, 0:HALF], "sv")
+        front_small(aw_raw, wa[:], was[:], "sv")
+        mm1(0)
+        front_x(0, "svsv")
+        front_small(q_raw[0], gc[:, 1024:1536], gs[:, 1024:1536], "sv")
+        m0 = mpool.tile([P, 8, HALF], F32, tag="mT")
+        for i in range(4):
+            front_w(i, "ssss")
+            gating(0, i, 0, m0)
+            gating(0, i, 1, m0)
+        front_small(c_raw[1], cc[:, HALF:T], cs[:, HALF:T], "ss")
+        mm1(1)
+        front_x(1, "ssss")
+        front_small(q_raw[1], gc[:, 1536 + 1024 : 3072], gs[:, 1536 + 1024 : 3072], "ss")
+        m1 = mpool.tile([P, 8, HALF], F32, tag="mT")
+        for i in range(4):
+            gating(1, i, 0, m1)
+            gating(1, i, 1, m1)
+            layernorm(0, i, m0)
+        for j in range(4):
+            layernorm(1, j, m1)

@@ -39,16 +39,9 @@ def tile_rotelearningmemory_pa_kernel(
 
     with ExitStack() as stack:
         keep = stack.enter_context(tc.tile_pool(name="keep", bufs=1))
-        actraw = stack.enter_context(tc.tile_pool(name="actraw", bufs=4))
-        wraw = stack.enter_context(tc.tile_pool(name="wraw", bufs=2))
-        grp = stack.enter_context(tc.tile_pool(name="grp", bufs=3))
-        grpw = stack.enter_context(tc.tile_pool(name="grpw", bufs=2))
-        rpool = stack.enter_context(tc.tile_pool(name="rpool", bufs=1))
-        mpool = stack.enter_context(tc.tile_pool(name="mpool", bufs=2))
-        work = stack.enter_context(tc.tile_pool(name="work", bufs=2))
+        gwork = stack.enter_context(tc.tile_pool(name="gwork", bufs=3))
         small = stack.enter_context(tc.tile_pool(name="small", bufs=4))
-        psum = stack.enter_context(tc.psum_pool(name="psum", bufs=2))
-
+        psum = stack.enter_context(tc.psum_pool(name="psum", bufs=8))
         ident_f = keep.tile([P, P], F32)
         make_identity(nc, ident_f[:])
         ident_b = keep.tile([P, P], BF16)
@@ -62,40 +55,6 @@ def tile_rotelearningmemory_pa_kernel(
         vec = keep.tile([P, 256], BF16)
         nc.vector.memset(vec[:].bitcast(F32), 0.0)
 
-        nc.scalar.dma_start(out=vec[8:10, :], in_=attn_out_b.rearrange("(r c) -> r c", c=256))
-        nc.scalar.dma_start(out=vec[0:4, :], in_=gate_b.rearrange("(r c) -> r c", c=256))
-        nc.scalar.dma_start(out=vec[4:8, :], in_=op_b.rearrange("(r c) -> r c", c=256))
-
-        x_raw = keep.tile([P, 4, 2 * D], BF16)
-        c_raw = []
-        q_raw = []
-        gw_raw = []
-        ow_raw = []
-
-        def load_act(src, th, nm):
-            t = actraw.tile([P, 2, 2 * M], BF16, name=nm, tag="act")
-            nc.sync.dma_start(out=t[:], in_=src[:, 2 * th : 2 * th + 2, :])
-            return t
-
-        c_raw.append(load_act(c_d, 0, "c_raw0"))
-        aw_raw = load_act(aw_d, 0, "aw_raw")
-        nc.sync.dma_start(out=x_raw[:, 0:2, :], in_=x_d[:, 0:2, :])
-        q_raw.append(load_act(q_d, 0, "q_raw0"))
-        for i in range(4):
-            g_t = wraw.tile([P, 2 * (D + M)], BF16, name="gw_raw%d" % i, tag="gwraw")
-            nc.sync.dma_start(out=g_t[:], in_=gw_d[:, i, :])
-            gw_raw.append(g_t)
-            o_t = wraw.tile([P, 2 * M], BF16, name="ow_raw%d" % i, tag="owraw")
-            nc.sync.dma_start(out=o_t[:], in_=ow_d[:, i, :])
-            ow_raw.append(o_t)
-        c_raw.append(load_act(c_d, 1, "c_raw1"))
-        nc.sync.dma_start(out=x_raw[:, 2:4, :], in_=x_d[:, 2:4, :])
-        q_raw.append(load_act(q_d, 1, "q_raw1"))
-        lg_bc = keep.tile([P, D], BF16)
-        nc.scalar.dma_start(out=lg_bc[:], in_=ln_g.partition_broadcast(P))
-        lb_bc = keep.tile([P, D], BF16)
-        nc.scalar.dma_start(out=lb_bc[:], in_=ln_b.partition_broadcast(P))
-
         cc = keep.tile([P, T], U32, align_bytes=64)
         cs = keep.tile([P, T], U8, align_bytes=64)
         wa = keep.tile([P, M], U32, align_bytes=64)
@@ -108,11 +67,13 @@ def tile_rotelearningmemory_pa_kernel(
         rs = keep.tile([P, T], U8, align_bytes=64)
         gx = keep.tile([P, 2 * 2 * HALF * 4], BF16, align_bytes=64)
 
+        m0 = keep.tile([P, 8, HALF], F32)
+
         def words(t3):
             return t3[:].rearrange("p i k -> p (i k)").bitcast(F32)
 
         def bank(src_words, base, row_words, dst_bf16, eng):
-            tp = psum.tile([P, 2, 256], F32, tag="tp")
+            tp = psum.tile([P, 2, 256], F32, tag="bank")
             for u in range(2):
                 for e in range(2):
                     o = base + e * row_words + u * P
@@ -133,92 +94,159 @@ def tile_rotelearningmemory_pa_kernel(
                 start=start, stop=stop,
             )
 
-        vt = psum.tile([P, 2, 256], F32, tag="tp")
-        nc.tensor.transpose(vt[:, 0, 0:P], vec[:].bitcast(F32), ident_f[:])
-        vt_b = vt[:, 0, 0:16].bitcast(BF16)
-        ngb = keep.tile([P, 8], F32)
-        nc.vector.tensor_scalar_mul(out=ngb[:], in0=vt_b[:, 0:8], scalar1=-1.0)
-        ob = keep.tile([P, 8], F32)
-        nc.vector.tensor_copy(out=ob[:], in_=vt_b[:, 8:16])
-        ab = keep.tile([P, 4], F32)
-        nc.vector.tensor_copy(out=ab[:], in_=vt_b[:, 16:20])
-
-        def front_small(raw_t, codes, scales, engs):
-            g = grp.tile([P, 4 * HALF], BF16, tag="ga", align_bytes=64)
-            w = words(raw_t)
-            for il in range(2):
-                bank(w, il * M, M // 2, g[:, il * 1024 : (il + 1) * 1024], engs[il])
-            quant(g[:], codes, scales)
-
-        def front_x(th, engs):
-            w = words(x_raw)
-            n = 0
-            for g in range(2):
-                for il in range(2):
-                    a = ((th * 2 + g) * HALF + il * 256) * 4
-                    bank(w, (2 * th + il) * D + g * 256, D // 2, gx[:, a : a + 1024], engs[n])
-                    n += 1
-            quant(
-                gx[:, th * 4096 : (th + 1) * 4096],
-                gc[:, th * 1536 : th * 1536 + 1024],
-                gs[:, th * 1536 : th * 1536 + 1024],
-            )
-
-        def front_w(i, engs):
-            g = grpw.tile([P, 4 * 4 * 256], BF16, tag="gw", align_bytes=64)
-            gww = gw_raw[i][:].bitcast(F32)
-            for s in range(3):
-                bank(gww, s * 256, (D + M) // 2, g[:, s * 1024 : (s + 1) * 1024], engs[s])
-            bank(ow_raw[i][:].bitcast(F32), 0, M // 2, g[:, 3072:4096], engs[3])
-            quant(g[:], wc[:, i * 1024 : (i + 1) * 1024], ws[:, i * 1024 : (i + 1) * 1024])
-
-        def mm1(th):
-            r_t = rpool.tile([P, 4, HALF], BF16, tag="rT")
-            for t in range(4):
-                p1 = psum.tile([P, HALF], F32, name="p1_%d_%d" % (th, t), tag=("p3" if t % 2 == 0 else "p2"))
-                mx(
-                    p1[:], wa[:, t * P : (t + 1) * P], was[:, t * P : (t + 1) * P],
-                    cc[:, th * HALF : (th + 1) * HALF], cs[:, th * HALF : (th + 1) * HALF], True, True,
-                )
-                nc.scalar.activation(out=r_t[:, t, :], in_=p1[:], func=ACT.Identity, bias=ab[:, t : t + 1], scale=1.0)
-            g_r = rpool.tile([P, HALF, 4], BF16, tag="gr", align_bytes=64)
-            nc.vector.tensor_copy(out=g_r[:], in_=r_t[:].rearrange("p t c -> p c t"))
-            quant(
-                g_r[:].rearrange("p c t -> p (c t)"),
-                rc[:, th * HALF : (th + 1) * HALF], rs[:, th * HALF : (th + 1) * HALF],
-            )
-
         gx5 = gx[:].rearrange("p (h g c t) -> p h g c t", h=2, g=2, t=4)
 
         def gating(th, i, e, m_t):
             d = 2 * i + e
-            p3 = psum.tile([P, HALF], F32, tag="p3")
+            p3 = psum.tile([P, HALF], F32, tag="bank")
             for s in range(3):
                 a = (i * 4 + s) * 256 + e * P
                 b = (th * 3 + s) * HALF
                 mx(p3[:], wc[:, a : a + P], ws[:, a : a + P], gc[:, b : b + HALF], gs[:, b : b + HALF], s == 0, s == 2)
-            p2 = psum.tile([P, HALF], F32, tag="p2")
+            p2 = psum.tile([P, HALF], F32, tag="bank")
             a = (i * 4 + 3) * 256 + e * P
             mx(
                 p2[:], wc[:, a : a + P], ws[:, a : a + P],
                 rc[:, th * HALF : (th + 1) * HALF], rs[:, th * HALF : (th + 1) * HALF], True, True,
             )
-            h_t = work.tile([P, HALF], F32, tag="h")
+            h_t = gwork.tile([P, HALF], F32, tag="h")
             nc.scalar.activation(out=h_t[:], in_=p3[:], func=ACT.Sigmoid, bias=ngb[:, d : d + 1], scale=-1.0)
-            e_t = work.tile([P, HALF], F32, tag="e")
+            e_t = gwork.tile([P, HALF], F32, tag="e")
             nc.vector.scalar_tensor_tensor(
                 out=e_t[:], in0=p2[:], scalar=ob[:, d : d + 1], in1=gx5[:, th, i // 2, :, 2 * (i % 2) + e],
                 op0=ALU.add, op1=ALU.subtract,
             )
             nc.vector.tensor_tensor(out=m_t[:, d, :], in0=h_t[:], in1=e_t[:], op=ALU.mult)
 
+        with ExitStack() as front:
+            actraw = front.enter_context(tc.tile_pool(name="actraw", bufs=5))
+            wraw = front.enter_context(tc.tile_pool(name="wraw", bufs=4))
+            grp = front.enter_context(tc.tile_pool(name="grp", bufs=3))
+            grpw = front.enter_context(tc.tile_pool(name="grpw", bufs=2))
+            rpool = front.enter_context(tc.tile_pool(name="rpool", bufs=2))
+
+            nc.sync.dma_start(out=vec[8:10, :], in_=attn_out_b.rearrange("(r c) -> r c", c=256))
+            nc.sync.dma_start(out=vec[0:4, :], in_=gate_b.rearrange("(r c) -> r c", c=256))
+            nc.sync.dma_start(out=vec[4:8, :], in_=op_b.rearrange("(r c) -> r c", c=256))
+
+            x_raw = keep.tile([P, 4, 2 * D], BF16)
+            c_raw = []
+            q_raw = []
+            gw_raw = []
+            ow_raw = []
+
+            def load_act(src, th, nm):
+                t = actraw.tile([P, 2, 2 * M], BF16, name=nm, tag="act")
+                nc.sync.dma_start(out=t[:], in_=src[:, 2 * th : 2 * th + 2, :])
+                return t
+
+            c_raw.append(load_act(c_d, 0, "c_raw0"))
+            aw_raw = load_act(aw_d, 0, "aw_raw")
+            nc.sync.dma_start(out=x_raw[:, 0:2, :], in_=x_d[:, 0:2, :])
+            q_raw.append(load_act(q_d, 0, "q_raw0"))
+            for i in range(4):
+                g_t = wraw.tile([P, 2 * (D + M)], BF16, name="gw_raw%d" % i, tag="gwraw")
+                nc.sync.dma_start(out=g_t[:], in_=gw_d[:, i, :])
+                gw_raw.append(g_t)
+                o_t = wraw.tile([P, 2 * M], BF16, name="ow_raw%d" % i, tag="owraw")
+                nc.sync.dma_start(out=o_t[:], in_=ow_d[:, i, :])
+                ow_raw.append(o_t)
+            c_raw.append(load_act(c_d, 1, "c_raw1"))
+            nc.sync.dma_start(out=x_raw[:, 2:4, :], in_=x_d[:, 2:4, :])
+            q_raw.append(load_act(q_d, 1, "q_raw1"))
+            lg_bc = keep.tile([P, D], BF16)
+            nc.sync.dma_start(out=lg_bc[:], in_=ln_g.partition_broadcast(P))
+            lb_bc = keep.tile([P, D], BF16)
+            nc.sync.dma_start(out=lb_bc[:], in_=ln_b.partition_broadcast(P))
+
+            def front_small(raw_t, codes, scales, engs):
+                g = grp.tile([P, 4 * HALF], BF16, tag="ga", align_bytes=64)
+                w = words(raw_t)
+                for il in range(2):
+                    bank(w, il * M, M // 2, g[:, il * 1024 : (il + 1) * 1024], engs[il])
+                quant(g[:], codes, scales)
+
+            def front_x(th, engs):
+                w = words(x_raw)
+                n = 0
+                for g in range(2):
+                    for il in range(2):
+                        a = ((th * 2 + g) * HALF + il * 256) * 4
+                        bank(w, (2 * th + il) * D + g * 256, D // 2, gx[:, a : a + 1024], engs[n])
+                        n += 1
+                quant(
+                    gx[:, th * 4096 : (th + 1) * 4096],
+                    gc[:, th * 1536 : th * 1536 + 1024],
+                    gs[:, th * 1536 : th * 1536 + 1024],
+                )
+
+            def front_w(i, engs):
+                g = grpw.tile([P, 4 * 4 * 256], BF16, tag="gw", align_bytes=64)
+                gww = gw_raw[i][:].bitcast(F32)
+                for s in range(3):
+                    bank(gww, s * 256, (D + M) // 2, g[:, s * 1024 : (s + 1) * 1024], engs[s])
+                bank(ow_raw[i][:].bitcast(F32), 0, M // 2, g[:, 3072:4096], engs[3])
+                quant(g[:], wc[:, i * 1024 : (i + 1) * 1024], ws[:, i * 1024 : (i + 1) * 1024])
+
+            def mm1(th):
+                r_t = rpool.tile([P, 4, HALF], BF16, tag="rT")
+                for t in range(4):
+                    p1 = psum.tile([P, HALF], F32, name="p1_%d_%d" % (th, t), tag="bank")
+                    mx(
+                        p1[:], wa[:, t * P : (t + 1) * P], was[:, t * P : (t + 1) * P],
+                        cc[:, th * HALF : (th + 1) * HALF], cs[:, th * HALF : (th + 1) * HALF], True, True,
+                    )
+                    nc.scalar.activation(out=r_t[:, t, :], in_=p1[:], func=ACT.Identity, bias=ab[:, t : t + 1], scale=1.0)
+                g_r = rpool.tile([P, HALF, 4], BF16, tag="gr", align_bytes=64)
+                nc.vector.tensor_copy(out=g_r[:], in_=r_t[:].rearrange("p t c -> p c t"))
+                quant(
+                    g_r[:].rearrange("p c t -> p (c t)"),
+                    rc[:, th * HALF : (th + 1) * HALF], rs[:, th * HALF : (th + 1) * HALF],
+                )
+
+            front_small(c_raw[0], cc[:, 0:HALF], cs[:, 0:HALF], "sv")
+            front_small(aw_raw, wa[:], was[:], "sv")
+
+            vt = psum.tile([P, 2, 256], F32, tag="bank")
+            nc.tensor.transpose(vt[:, 0, 0:P], vec[:].bitcast(F32), ident_f[:])
+            vt_b = vt[:, 0, 0:16].bitcast(BF16)
+            ngb = keep.tile([P, 8], F32)
+            nc.vector.tensor_scalar_mul(out=ngb[:], in0=vt_b[:, 0:8], scalar1=-1.0)
+            ob = keep.tile([P, 8], F32)
+            nc.vector.tensor_copy(out=ob[:], in_=vt_b[:, 8:16])
+            ab = keep.tile([P, 4], F32)
+            nc.vector.tensor_copy(out=ab[:], in_=vt_b[:, 16:20])
+
+            mm1(0)
+            front_x(0, "svsv")
+            front_small(q_raw[0], gc[:, 1024:1536], gs[:, 1024:1536], "sv")
+            front_w(0, "ssss")
+            front_w(1, "ssss")
+            for i in range(4):
+                gating(0, i, 0, m0)
+                gating(0, i, 1, m0)
+                if i < 2:
+                    front_w(i + 2, "ssss")
+                if i == 1:
+                    front_small(c_raw[1], cc[:, HALF:T], cs[:, HALF:T], "ss")
+                    mm1(1)
+                if i == 2:
+                    front_x(1, "ssss")
+                if i == 3:
+                    front_small(q_raw[1], gc[:, 1536 + 1024 : 3072], gs[:, 1536 + 1024 : 3072], "ss")
+
+        late = stack.enter_context(tc.tile_pool(name="late", bufs=1))
+        lny = stack.enter_context(tc.tile_pool(name="lny", bufs=4))
+        lnw = stack.enter_context(tc.tile_pool(name="lnw", bufs=3))
+        m1 = late.tile([P, 8, HALF], F32)
+
         def layernorm(th, j, m_t):
             i_tok = 2 * th + j // 2
             e_tok = j % 2
-            y_t = work.tile([P, D], F32, tag="y")
+            y_t = lny.tile([P, D], F32, tag="y")
             s1 = small.tile([P, 2], F32, tag="s1")
             for g in range(2):
-                yp = psum.tile([P, 2, 256], F32, tag="y")
+                yp = psum.tile([P, 2, 256], F32, tag="bank")
                 nc.tensor.matmul(
                     out=yp[:], lhsT=ident_b[:],
                     rhs=x_raw[:, i_tok, e_tok * D + g * 512 : e_tok * D + (g + 1) * 512].rearrange("p (a e) -> p e a", e=2),
@@ -238,10 +266,10 @@ def tile_rotelearningmemory_pa_kernel(
             nc.gpsimd.tensor_scalar(
                 out=nmean[:], in0=s1[:, 0:1], scalar1=s1[:, 1:2], scalar2=-1.0 / D, op0=ALU.add, op1=ALU.mult
             )
-            junk = work.tile([P, D], BF16, tag="junk")
+            junk = late.tile([P, D], BF16, tag="junk")
             s2 = small.tile([P, 1], F32, tag="s2")
             nc.scalar.activation(out=junk[:], in_=y_t[:], func=ACT.Square, bias=nmean[:], scale=1.0, accum_out=s2[:])
-            w_t = work.tile([P, D], F32, tag="w")
+            w_t = lnw.tile([P, D], F32, tag="w")
             nc.vector.scalar_tensor_tensor(
                 out=w_t[:], in0=y_t[:], scalar=nmean[:], in1=lg_bc[:], op0=ALU.add, op1=ALU.mult
             )
@@ -249,27 +277,12 @@ def tile_rotelearningmemory_pa_kernel(
             nc.gpsimd.tensor_scalar(out=ve[:], in0=s2[:], scalar1=1.0 / D, scalar2=LN_EPS, op0=ALU.mult, op1=ALU.add)
             rstd = small.tile([P, 1], F32, tag="rstd")
             nc.gpsimd.tensor_tensor(out=rstd[:], in0=ve[:], in1=mhalf[:], op=ALU.pow)
-            o_t = work.tile([P, D], F32, tag="o")
+            o_t = lny.tile([P, D], F32, tag="o")
             nc.vector.scalar_tensor_tensor(
                 out=o_t[:], in0=w_t[:], scalar=rstd[:], in1=lb_bc[:], op0=ALU.mult, op1=ALU.add
             )
             nc.sync.dma_start(out=out_d[:, i_tok, e_tok, :], in_=o_t[:])
 
-        front_small(c_raw[0], cc[:, 0:HALF], cs[:, 0:HALF], "sv")
-        front_small(aw_raw, wa[:], was[:], "sv")
-        mm1(0)
-        front_x(0, "svsv")
-        front_small(q_raw[0], gc[:, 1024:1536], gs[:, 1024:1536], "sv")
-        m0 = mpool.tile([P, 8, HALF], F32, tag="mT")
-        for i in range(4):
-            front_w(i, "ssss")
-            gating(0, i, 0, m0)
-            gating(0, i, 1, m0)
-        front_small(c_raw[1], cc[:, HALF:T], cs[:, HALF:T], "ss")
-        mm1(1)
-        front_x(1, "ssss")
-        front_small(q_raw[1], gc[:, 1536 + 1024 : 3072], gs[:, 1536 + 1024 : 3072], "ss")
-        m1 = mpool.tile([P, 8, HALF], F32, tag="mT")
         for i in range(4):
             gating(1, i, 0, m1)
             gating(1, i, 1, m1)

@@ -239,14 +239,18 @@ def tile_rotelearningmemory_pa_kernel(
         lny = stack.enter_context(tc.tile_pool(name="lny", bufs=4))
         lnw = stack.enter_context(tc.tile_pool(name="lnw", bufs=3))
         m1 = late.tile([P, 8, HALF], F32)
+        lg32 = late.tile([P, D], BF16)
+        nc.vector.tensor_scalar_mul(out=lg32[:], in0=lg_bc[:], scalar1=32.0)
 
         def layernorm(th, j, m_t):
             i_tok = 2 * th + j // 2
             e_tok = j % 2
             y_t = lny.tile([P, D], F32, tag="y")
             s1 = small.tile([P, 2], F32, tag="s1")
+            banks = []
             for g in range(2):
-                yp = psum.tile([P, 2, 256], F32, tag="bank")
+                yp = psum.tile([P, 2, 256], F32, name="yp%d" % g, tag="bank")
+                banks.append(yp)
                 nc.tensor.matmul(
                     out=yp[:], lhsT=ident_b[:],
                     rhs=x_raw[:, i_tok, e_tok * D + g * 512 : e_tok * D + (g + 1) * 512].rearrange("p (a e) -> p e a", e=2),
@@ -262,24 +266,28 @@ def tile_rotelearningmemory_pa_kernel(
                     out=y_t[:, g * 512 : (g + 1) * 512].rearrange("p (a e) -> p a e", e=2),
                     in_=yp[:].rearrange("p e a -> p a e"), func=ACT.Identity, accum_out=s1[:, g : g + 1],
                 )
+            tot = small.tile([P, 1], F32, tag="tot")
+            nc.scalar.activation(out=tot[:], in_=s1[:, 0:1], func=ACT.Identity, bias=s1[:, 1:2], scale=1.0)
             nmean = small.tile([P, 1], F32, tag="nmean")
-            nc.gpsimd.tensor_scalar(
-                out=nmean[:], in0=s1[:, 0:1], scalar1=s1[:, 1:2], scalar2=-1.0 / D, op0=ALU.add, op1=ALU.mult
-            )
+            nc.scalar.mul(out=nmean[:], in_=tot[:], mul=-1.0 / D)
             junk = late.tile([P, D], BF16, tag="junk")
             s2 = small.tile([P, 1], F32, tag="s2")
             nc.scalar.activation(out=junk[:], in_=y_t[:], func=ACT.Square, bias=nmean[:], scale=1.0, accum_out=s2[:])
-            w_t = lnw.tile([P, D], F32, tag="w")
-            nc.vector.scalar_tensor_tensor(
-                out=w_t[:], in0=y_t[:], scalar=nmean[:], in1=lg_bc[:], op0=ALU.add, op1=ALU.mult
-            )
             ve = small.tile([P, 1], F32, tag="ve")
-            nc.gpsimd.tensor_scalar(out=ve[:], in0=s2[:], scalar1=1.0 / D, scalar2=LN_EPS, op0=ALU.mult, op1=ALU.add)
-            rstd = small.tile([P, 1], F32, tag="rstd")
-            nc.gpsimd.tensor_tensor(out=rstd[:], in0=ve[:], in1=mhalf[:], op=ALU.pow)
+            nc.scalar.add(out=ve[:], in_=s2[:], add=D * LN_EPS)
+            w_t = lnw.tile([P, D], F32, tag="w")
+            for g in range(2):
+                nc.vector.scalar_tensor_tensor(
+                    out=w_t[:, g * 512 : (g + 1) * 512].rearrange("p (a e) -> p a e", e=2),
+                    in0=banks[g][:].rearrange("p e a -> p a e"), scalar=nmean[:],
+                    in1=lg32[:, g * 512 : (g + 1) * 512].rearrange("p (a e) -> p a e", e=2),
+                    op0=ALU.add, op1=ALU.mult,
+                )
+            rs32 = small.tile([P, 1], F32, tag="rs32")
+            nc.gpsimd.tensor_tensor(out=rs32[:], in0=ve[:], in1=mhalf[:], op=ALU.pow)
             o_t = lny.tile([P, D], F32, tag="o")
             nc.vector.scalar_tensor_tensor(
-                out=o_t[:], in0=w_t[:], scalar=rstd[:], in1=lb_bc[:], op0=ALU.mult, op1=ALU.add
+                out=o_t[:], in0=w_t[:], scalar=rs32[:], in1=lb_bc[:], op0=ALU.mult, op1=ALU.add
             )
             nc.sync.dma_start(out=out_d[:, i_tok, e_tok, :], in_=o_t[:])
 

@@ -237,7 +237,8 @@ def tile_rotelearningmemory_pa_kernel(
 
         late = stack.enter_context(tc.tile_pool(name="late", bufs=1))
         lny = stack.enter_context(tc.tile_pool(name="lny", bufs=4))
-        lnw = stack.enter_context(tc.tile_pool(name="lnw", bufs=3))
+        lnw = stack.enter_context(tc.tile_pool(name="lnw", bufs=8))
+        small8 = stack.enter_context(tc.tile_pool(name="small8", bufs=8))
         m1 = late.tile([P, 8, HALF], F32)
         lg32 = late.tile([P, D], BF16)
         nc.vector.tensor_scalar_mul(out=lg32[:], in0=lg_bc[:], scalar1=32.0)
@@ -283,17 +284,25 @@ def tile_rotelearningmemory_pa_kernel(
                     in1=lg32[:, g * 512 : (g + 1) * 512].rearrange("p (a e) -> p a e", e=2),
                     op0=ALU.add, op1=ALU.mult,
                 )
-            rs32 = small.tile([P, 1], F32, tag="rs32")
+            rs32 = small8.tile([P, 1], F32, tag="rs32")
             nc.gpsimd.tensor_tensor(out=rs32[:], in0=ve[:], in1=mhalf[:], op=ALU.pow)
+            return w_t, rs32
+
+        def layernorm_out(th, j, w_t, rs32):
+            i_tok = 2 * th + j // 2
+            e_tok = j % 2
             o_t = lny.tile([P, D], F32, tag="o")
             nc.vector.scalar_tensor_tensor(
                 out=o_t[:], in0=w_t[:], scalar=rs32[:], in1=lb_bc[:], op0=ALU.mult, op1=ALU.add
             )
             nc.sync.dma_start(out=out_d[:, i_tok, e_tok, :], in_=o_t[:])
 
+        pending = []
         for i in range(4):
             gating(1, i, 0, m1)
             gating(1, i, 1, m1)
-            layernorm(0, i, m0)
+            pending.append((0, i) + layernorm(0, i, m0))
         for j in range(4):
-            layernorm(1, j, m1)
+            pending.append((1, j) + layernorm(1, j, m1))
+        for th, j, w_t, rs32 in pending:
+            layernorm_out(th, j, w_t, rs32)

@@ -142,6 +142,7 @@ def tile_rotelearningmemory_pa_kernel(
 
             c_raw.append(load_act(c_d, 0, "c_raw0"))
             aw_raw = load_act(aw_d, 0, "aw_raw")
+            c_raw.append(load_act(c_d, 1, "c_raw1"))
             nc.sync.dma_start(out=x_raw[:, 0:2, :], in_=x_d[:, 0:2, :])
             q_raw.append(load_act(q_d, 0, "q_raw0"))
             for i in range(4):
@@ -151,7 +152,6 @@ def tile_rotelearningmemory_pa_kernel(
                 o_t = wraw.tile([P, 2 * M], BF16, name="ow_raw%d" % i, tag="owraw")
                 nc.sync.dma_start(out=o_t[:], in_=ow_d[:, i, :])
                 ow_raw.append(o_t)
-            c_raw.append(load_act(c_d, 1, "c_raw1"))
             nc.sync.dma_start(out=x_raw[:, 2:4, :], in_=x_d[:, 2:4, :])
             q_raw.append(load_act(q_d, 1, "q_raw1"))
             lg_bc = keep.tile([P, D], BF16)
@@ -218,6 +218,8 @@ def tile_rotelearningmemory_pa_kernel(
             nc.vector.tensor_copy(out=ab[:], in_=vt_b[:, 16:20])
 
             mm1(0)
+            front_small(c_raw[1], cc[:, HALF:T], cs[:, HALF:T], "sv")
+            mm1(1)
             front_x(0, "svsv")
             front_small(q_raw[0], gc[:, 1024:1536], gs[:, 1024:1536], "sv")
             front_w(0, "ssss")
@@ -227,9 +229,6 @@ def tile_rotelearningmemory_pa_kernel(
                 gating(0, i, 1, m0)
                 if i < 2:
                     front_w(i + 2, "ssss")
-                if i == 1:
-                    front_small(c_raw[1], cc[:, HALF:T], cs[:, HALF:T], "ss")
-                    mm1(1)
                 if i == 2:
                     front_x(1, "ssss")
                 if i == 3:
@@ -292,10 +291,14 @@ def tile_rotelearningmemory_pa_kernel(
             i_tok = 2 * th + j // 2
             e_tok = j % 2
             o_t = lny.tile([P, D], F32, tag="o")
-            nc.vector.scalar_tensor_tensor(
-                out=o_t[:], in0=w_t[:], scalar=rs32[:], in1=lb_bc[:], op0=ALU.mult, op1=ALU.add
-            )
-            nc.sync.dma_start(out=out_d[:, i_tok, e_tok, :], in_=o_t[:])
+            pieces = 2 if (th == 1 and j == 3) else 1
+            width = D // pieces
+            for c in range(pieces):
+                cols = slice(c * width, (c + 1) * width)
+                nc.vector.scalar_tensor_tensor(
+                    out=o_t[:, cols], in0=w_t[:, cols], scalar=rs32[:], in1=lb_bc[:, cols], op0=ALU.mult, op1=ALU.add
+                )
+                nc.sync.dma_start(out=out_d[:, i_tok, e_tok, cols], in_=o_t[:, cols])
 
         pending = []
         for i in range(4):

@@ -96,27 +96,26 @@ def tile_rotelearningmemory_pa_kernel(
 
         gx5 = gx[:].rearrange("p (h g c t) -> p h g c t", h=2, g=2, t=4)
 
-        def gating(th, i, e, m_t):
-            d = 2 * i + e
-            p3 = psum.tile([P, HALF], F32, tag="bank")
-            for s in range(3):
-                a = (i * 4 + s) * 256 + e * P
-                b = (th * 3 + s) * HALF
-                mx(p3[:], wc[:, a : a + P], ws[:, a : a + P], gc[:, b : b + HALF], gs[:, b : b + HALF], s == 0, s == 2)
-            p2 = psum.tile([P, HALF], F32, tag="bank")
-            a = (i * 4 + 3) * 256 + e * P
-            mx(
-                p2[:], wc[:, a : a + P], ws[:, a : a + P],
-                rc[:, th * HALF : (th + 1) * HALF], rs[:, th * HALF : (th + 1) * HALF], True, True,
-            )
-            h_t = gwork.tile([P, HALF], F32, tag="h")
-            nc.scalar.activation(out=h_t[:], in_=p3[:], func=ACT.Sigmoid, bias=ngb[:, d : d + 1], scale=-1.0)
-            e_t = gwork.tile([P, HALF], F32, tag="e")
-            nc.vector.scalar_tensor_tensor(
-                out=e_t[:], in0=p2[:], scalar=ob[:, d : d + 1], in1=gx5[:, th, i // 2, :, 2 * (i % 2) + e],
-                op0=ALU.add, op1=ALU.subtract,
-            )
-            nc.vector.tensor_tensor(out=m_t[:, d, :], in0=h_t[:], in1=e_t[:], op=ALU.mult)
+        def gating(th, i, m_t):
+            tok = slice(th * HALF, (th + 1) * HALF)
+            h_t = gwork.tile([P, 2, HALF], F32, tag="h")
+            e_t = gwork.tile([P, 2, HALF], F32, tag="e")
+            for e in range(2):
+                d = 2 * i + e
+                p2 = psum.tile([P, HALF], F32, name="p2_%d" % e, tag="bank")
+                a = (i * 4 + 3) * 256 + e * P
+                mx(p2[:], wc[:, a : a + P], ws[:, a : a + P], rc[:, tok], rs[:, tok], True, True)
+                p3 = psum.tile([P, HALF], F32, name="p3_%d" % e, tag="bank")
+                for s in range(3):
+                    a = (i * 4 + s) * 256 + e * P
+                    b = (th * 3 + s) * HALF
+                    mx(p3[:], wc[:, a : a + P], ws[:, a : a + P], gc[:, b : b + HALF], gs[:, b : b + HALF], s == 0, s == 2)
+                nc.scalar.activation(out=h_t[:, e, :], in_=p3[:], func=ACT.Sigmoid, bias=ngb[:, d : d + 1], scale=-1.0)
+                nc.vector.scalar_tensor_tensor(
+                    out=e_t[:, e, :], in0=p2[:], scalar=ob[:, d : d + 1], in1=gx5[:, th, i // 2, :, 2 * (i % 2) + e],
+                    op0=ALU.add, op1=ALU.subtract,
+                )
+            nc.vector.tensor_tensor(out=m_t[:, 2 * i : 2 * i + 2, :], in0=h_t[:], in1=e_t[:], op=ALU.mult)
 
         with ExitStack() as front:
             actraw = front.enter_context(tc.tile_pool(name="actraw", bufs=5))
@@ -198,7 +197,9 @@ def tile_rotelearningmemory_pa_kernel(
                     )
                     nc.scalar.activation(out=r_t[:, t, :], in_=p1[:], func=ACT.Identity, bias=ab[:, t : t + 1], scale=1.0)
                 g_r = rpool.tile([P, HALF, 4], BF16, tag="gr", align_bytes=64)
-                nc.vector.tensor_copy(out=g_r[:], in_=r_t[:].rearrange("p t c -> p c t"))
+                nc.vector.tensor_copy(
+                    out=g_r[:].rearrange("p (c i) t -> p c t i", i=4), in_=r_t[:].rearrange("p t (c i) -> p c t i", i=4)
+                )
                 quant(
                     g_r[:].rearrange("p c t -> p (c t)"),
                     rc[:, th * HALF : (th + 1) * HALF], rs[:, th * HALF : (th + 1) * HALF],
@@ -225,8 +226,7 @@ def tile_rotelearningmemory_pa_kernel(
             front_w(0, "ssss")
             front_w(1, "ssss")
             for i in range(4):
-                gating(0, i, 0, m0)
-                gating(0, i, 1, m0)
+                gating(0, i, m0)
                 if i < 2:
                     front_w(i + 2, "ssss")
                 if i == 2:
@@ -302,8 +302,7 @@ def tile_rotelearningmemory_pa_kernel(
 
         pending = []
         for i in range(4):
-            gating(1, i, 0, m1)
-            gating(1, i, 1, m1)
+            gating(1, i, m1)
             pending.append((0, i) + layernorm(0, i, m0))
         for j in range(4):
             pending.append((1, j) + layernorm(1, j, m1))

@@ -263,16 +263,16 @@ def tile_rotelearningmemory_pa_kernel(
                             rhs=ident_f[:], is_transpose=True, start=False, stop=(e == 1 and u == 1),
                         )
                 nc.scalar.activation(
-                    out=y_t[:, g * 512 : (g + 1) * 512].rearrange("p (a e) -> p a e", e=2),
-                    in_=yp[:].rearrange("p e a -> p a e"), func=ACT.Identity, accum_out=s1[:, g : g + 1],
+                    out=y_t[:, g * 512 : (g + 1) * 512], in_=yp[:].rearrange("p e a -> p (e a)"),
+                    func=ACT.Identity, scale=-1.0 / D, accum_out=s1[:, g : g + 1],
                 )
-            tot = small.tile([P, 1], F32, tag="tot")
-            nc.scalar.activation(out=tot[:], in_=s1[:, 0:1], func=ACT.Identity, bias=s1[:, 1:2], scale=1.0)
             nmean = small.tile([P, 1], F32, tag="nmean")
-            nc.scalar.mul(out=nmean[:], in_=tot[:], mul=-1.0 / D)
+            nc.scalar.activation(out=nmean[:], in_=s1[:, 0:1], func=ACT.Identity, bias=s1[:, 1:2], scale=1.0)
             junk = late.tile([P, D], BF16, tag="junk")
             s2 = small.tile([P, 1], F32, tag="s2")
-            nc.scalar.activation(out=junk[:], in_=y_t[:], func=ACT.Square, bias=nmean[:], scale=1.0, accum_out=s2[:])
+            nc.scalar.activation(
+                out=junk[:], in_=y_t[:], func=ACT.Square, bias=nmean[:], scale=-1.0 * D, accum_out=s2[:]
+            )
             ve = small.tile([P, 1], F32, tag="ve")
             nc.scalar.add(out=ve[:], in_=s2[:], add=D * LN_EPS)
             w_t = lnw.tile([P, D], F32, tag="w")

@@ -242,11 +242,9 @@ def tile_rotelearningmemory_pa_kernel(
         lg32 = late.tile([P, D], BF16)
         nc.vector.tensor_scalar_mul(out=lg32[:], in0=lg_bc[:], scalar1=32.0)
 
-        def layernorm(th, j, m_t):
+        def layernorm(th, j, m_t, on_vector):
             i_tok = 2 * th + j // 2
             e_tok = j % 2
-            y_t = lny.tile([P, D], F32, tag="y")
-            s1 = small.tile([P, 2], F32, tag="s1")
             banks = []
             for g in range(2):
                 yp = psum.tile([P, 2, 256], F32, name="yp%d" % g, tag="bank")
@@ -262,19 +260,33 @@ def tile_rotelearningmemory_pa_kernel(
                             out=yp[:, e, u * P : (u + 1) * P], lhsT=m_t[:, 2 * (2 * g + u) + e, j * P : (j + 1) * P],
                             rhs=ident_f[:], is_transpose=True, start=False, stop=(e == 1 and u == 1),
                         )
-                nc.scalar.activation(
-                    out=y_t[:, g * 512 : (g + 1) * 512], in_=yp[:].rearrange("p e a -> p (e a)"),
-                    func=ACT.Identity, scale=-1.0 / D, accum_out=s1[:, g : g + 1],
-                )
             nmean = small.tile([P, 1], F32, tag="nmean")
-            nc.scalar.activation(out=nmean[:], in_=s1[:, 0:1], func=ACT.Identity, bias=s1[:, 1:2], scale=1.0)
-            junk = late.tile([P, D], BF16, tag="junk")
-            s2 = small.tile([P, 1], F32, tag="s2")
-            nc.scalar.activation(
-                out=junk[:], in_=y_t[:], func=ACT.Square, bias=nmean[:], scale=-1.0 * D, accum_out=s2[:]
-            )
             ve = small.tile([P, 1], F32, tag="ve")
-            nc.scalar.add(out=ve[:], in_=s2[:], add=D * LN_EPS)
+            if on_vector:
+                stats = small.tile([P, 2, 6], F32, tag="stats")
+                for g in range(2):
+                    nc.vector.bn_stats(out=stats[:, g, :], in_=banks[g][:].rearrange("p e a -> p (e a)"))
+                mv = small.tile([P, 2], F32, tag="mv")
+                nc.vector.bn_aggr(out=mv[:], in_=stats[:].rearrange("p g s -> p (g s)"))
+                nc.vector.tensor_scalar_mul(out=nmean[:], in0=mv[:, 0:1], scalar1=-1.0)
+                nc.vector.tensor_scalar(
+                    out=ve[:], in0=mv[:, 1:2], scalar1=1.0 * D, scalar2=D * LN_EPS, op0=ALU.mult, op1=ALU.add
+                )
+            else:
+                y_t = lny.tile([P, D], F32, tag="y")
+                s1 = small.tile([P, 2], F32, tag="s1")
+                for g in range(2):
+                    nc.scalar.activation(
+                        out=y_t[:, g * 512 : (g + 1) * 512], in_=banks[g][:].rearrange("p e a -> p (e a)"),
+                        func=ACT.Identity, scale=-1.0 / D, accum_out=s1[:, g : g + 1],
+                    )
+                nc.scalar.activation(out=nmean[:], in_=s1[:, 0:1], func=ACT.Identity, bias=s1[:, 1:2], scale=1.0)
+                junk = late.tile([P, D], BF16, tag="junk")
+                s2 = small.tile([P, 1], F32, tag="s2")
+                nc.scalar.activation(
+                    out=junk[:], in_=y_t[:], func=ACT.Square, bias=nmean[:], scale=-1.0 * D, accum_out=s2[:]
+                )
+                nc.scalar.add(out=ve[:], in_=s2[:], add=D * LN_EPS)
             w_t = lnw.tile([P, D], F32, tag="w")
             for g in range(2):
                 nc.vector.scalar_tensor_tensor(
@@ -303,8 +315,8 @@ def tile_rotelearningmemory_pa_kernel(
         pending = []
         for i in range(4):
             gating(1, i, m1)
-            pending.append((0, i) + layernorm(0, i, m0))
+            pending.append((0, i) + layernorm(0, i, m0, False))
         for j in range(4):
-            pending.append((1, j) + layernorm(1, j, m1))
+            pending.append((1, j) + layernorm(1, j, m1, j == 3))
         for th, j, w_t, rs32 in pending:
             layernorm_out(th, j, w_t, rs32)

@@ -38,22 +38,15 @@ def tile_rotelearningmemory_pa_kernel(
     out_d = out.flatten_outer_dims().rearrange("(i q e) d -> q i e d", q=P, e=2)
 
     with ExitStack() as stack:
+        stack.enter_context(tc.manual_schedule())
         keep = stack.enter_context(tc.tile_pool(name="keep", bufs=1))
-        gwork = stack.enter_context(tc.tile_pool(name="gwork", bufs=3))
-        small = stack.enter_context(tc.tile_pool(name="small", bufs=4))
+        gwork = stack.enter_context(tc.tile_pool(name="gwork", bufs=4))
+        small = stack.enter_context(tc.tile_pool(name="small", bufs=8))
+        wraw = stack.enter_context(tc.tile_pool(name="wraw", bufs=3))
+        grp = stack.enter_context(tc.tile_pool(name="grp", bufs=3))
+        aux = stack.enter_context(tc.tile_pool(name="aux", bufs=2))
+        lnw = stack.enter_context(tc.tile_pool(name="lnw", bufs=4))
         psum = stack.enter_context(tc.psum_pool(name="psum", bufs=8))
-        ident_f = keep.tile([P, P], F32)
-        make_identity(nc, ident_f[:])
-        ident_b = keep.tile([P, P], BF16)
-        make_identity(nc, ident_b[:])
-        mhalf = keep.tile([P, 1], F32)
-        nc.gpsimd.memset(mhalf[:], -0.5)
-        warm_in = keep.tile([P, 1], F32)
-        nc.vector.memset(warm_in[:], 0.0)
-        warm_out = keep.tile([P, 1], F32)
-        nc.scalar.activation(out=warm_out[:], in_=warm_in[:], func=ACT.Sigmoid)
-        vec = keep.tile([P, 256], BF16)
-        nc.vector.memset(vec[:].bitcast(F32), 0.0)
 
         cc = keep.tile([P, T], U32, align_bytes=64)
         cs = keep.tile([P, T], U8, align_bytes=64)
@@ -66,18 +59,63 @@ def tile_rotelearningmemory_pa_kernel(
         rc = keep.tile([P, T], U32, align_bytes=64)
         rs = keep.tile([P, T], U8, align_bytes=64)
         gx = keep.tile([P, 2 * 2 * HALF * 4], BF16, align_bytes=64)
-
+        gx5 = gx[:].rearrange("p (h g c t) -> p h g c t", h=2, g=2, t=4)
         m0 = keep.tile([P, 8, HALF], F32)
+        m1 = keep.tile([P, 8, HALF], F32)
+        m_half = [m0, m1]
+        vec = keep.tile([P, 256], BF16)
+        x_raw = keep.tile([P, 4, 2 * D], BF16)
+        lg_bc = keep.tile([P, D], BF16)
+        lb_bc = keep.tile([P, D], BF16)
 
-        def words(t3):
-            return t3[:].rearrange("p i k -> p (i k)").bitcast(F32)
+        nc.vector.memset(vec[:].bitcast(F32), 0.0)
+        ident_f = keep.tile([P, P], F32)
+        make_identity(nc, ident_f[:])
+        ident_b = keep.tile([P, P], BF16)
+        make_identity(nc, ident_b[:])
+        mhalf = keep.tile([P, 1], F32)
+        nc.gpsimd.memset(mhalf[:], -0.5)
+        warm_in = keep.tile([P, 1], F32)
+        nc.vector.memset(warm_in[:], 0.0)
+        warm_out = keep.tile([P, 1], F32)
+        nc.scalar.activation(out=warm_out[:], in_=warm_in[:], func=ACT.Sigmoid)
 
-        def bank(src_words, base, row_words, dst_bf16, eng):
-            tp = psum.tile([P, 2, 256], F32, tag="bank")
+        def load_act(src, th, nm):
+            t = wraw.tile([P, 2, 2 * M], BF16, name=nm, tag="act")
+            nc.sync.dma_start(out=t[:], in_=src[:, 2 * th : 2 * th + 2, :])
+            return t
+
+        def load_w(i):
+            g_t = wraw.tile([P, 2 * (D + M)], BF16, name="gw_raw%d" % i, tag="gwraw")
+            nc.sync.dma_start(out=g_t[:], in_=gw_d[:, i, :])
+            o_t = wraw.tile([P, 2 * M], BF16, name="ow_raw%d" % i, tag="owraw")
+            nc.sync.dma_start(out=o_t[:], in_=ow_d[:, i, :])
+            return g_t, o_t
+
+        c_raw0 = load_act(c_d, 0, "c_raw0")
+        nc.sync.dma_start(out=vec[8:10, :], in_=attn_out_b.rearrange("(r c) -> r c", c=256))
+        nc.sync.dma_start(out=vec[0:4, :], in_=gate_b.rearrange("(r c) -> r c", c=256))
+        nc.sync.dma_start(out=vec[4:8, :], in_=op_b.rearrange("(r c) -> r c", c=256))
+        aw_raw = load_act(aw_d, 0, "aw_raw")
+        nc.sync.dma_start(out=x_raw[:, 0:2, :], in_=x_d[:, 0:2, :])
+        q_raw0 = load_act(q_d, 0, "q_raw0")
+        w_raw = [load_w(i) for i in range(2)]
+        c_raw1 = load_act(c_d, 1, "c_raw1")
+        w_raw += [load_w(i) for i in range(2, 4)]
+        nc.sync.dma_start(out=x_raw[:, 2:4, :], in_=x_d[:, 2:4, :])
+        q_raw1 = load_act(q_d, 1, "q_raw1")
+        nc.sync.dma_start(out=lg_bc[:], in_=ln_g.partition_broadcast(P))
+        nc.sync.dma_start(out=lb_bc[:], in_=ln_b.partition_broadcast(P))
+
+        def turn(words, base, row_words):
+            tp = psum.tile([P, 2, 256], F32, name="tp", tag="bank")
             for u in range(2):
                 for e in range(2):
                     o = base + e * row_words + u * P
-                    nc.tensor.transpose(tp[:, u, e * P : (e + 1) * P], src_words[:, o : o + P], ident_f[:])
+                    nc.tensor.transpose(tp[:, u, e * P : (e + 1) * P], words[:, o : o + P], ident_f[:])
+            return tp
+
+        def lay(tp, dst_bf16, eng):
             dst = dst_bf16.bitcast(F32).rearrange("p (r u) -> p r u", u=2)
             src = tp[:].rearrange("p u r -> p r u")
             if eng == "v":
@@ -94,229 +132,329 @@ def tile_rotelearningmemory_pa_kernel(
                 start=start, stop=stop,
             )
 
-        gx5 = gx[:].rearrange("p (h g c t) -> p h g c t", h=2, g=2, t=4)
+        def words(t3):
+            return t3[:].rearrange("p i k -> p (i k)").bitcast(F32)
 
-        def gating(th, i, m_t):
+        def small_turn(raw):
+            w = words(raw)
+            return [turn(w, il * M, M // 2) for il in range(2)]
+
+        def small_lay(tps, engs):
+            g = grp.tile([P, 4 * HALF], BF16, name="g_small", tag="ga", align_bytes=64)
+            for il in range(2):
+                lay(tps[il], g[:, il * 1024 : (il + 1) * 1024], engs[il])
+            return g
+
+        def x_turn(th, g):
+            w = words(x_raw)
+            return [turn(w, (2 * th + il) * D + g * 256, D // 2) for il in range(2)]
+
+        def x_lay(th, g, tps, engs):
+            for il in range(2):
+                a = ((th * 2 + g) * HALF + il * 256) * 4
+                lay(tps[il], gx[:, a : a + 1024], engs[il])
+
+        def x_quant(th, g):
+            a = th * 1536 + g * 512
+            quant(gx[:, (th * 2 + g) * 2048 : (th * 2 + g + 1) * 2048], gc[:, a : a + 512], gs[:, a : a + 512])
+
+        def q_quant(th, g):
+            a = th * 1536 + 1024
+            quant(g[:], gc[:, a : a + 512], gs[:, a : a + 512])
+
+        def w_turn(i):
+            g_t, o_t = w_raw[i]
+            tps = [turn(g_t[:].bitcast(F32), s * 256, (D + M) // 2) for s in range(3)]
+            tps.append(turn(o_t[:].bitcast(F32), 0, M // 2))
+            return tps
+
+        def w_tile():
+            g_w = grp.tile([P, 4 * 4 * 256], BF16, name="g_w", tag="gw", align_bytes=64)
+            return g_w
+
+        def w_lay(g, tps, s, eng):
+            lay(tps[s], g[:, s * 1024 : (s + 1) * 1024], eng)
+
+        def w_quant(i, g, h):
+            a = i * 1024 + h * 512
+            quant(g[:, h * 2048 : (h + 1) * 2048], wc[:, a : a + 512], ws[:, a : a + 512])
+
+        def mm1(th):
+            banks = []
+            for n in range(4):
+                p1 = psum.tile([P, 4, P], F32, name="p1", tag="bank")
+                c = slice(th * HALF + n * P, th * HALF + (n + 1) * P)
+                for t in range(4):
+                    mx(p1[:, t, :], wa[:, t * P : (t + 1) * P], was[:, t * P : (t + 1) * P], cc[:, c], cs[:, c], True, True)
+                banks.append(p1)
+            return banks
+
+        def r_tile():
+            g_r = grp.tile([P, HALF, 4], BF16, name="g_r", tag="ga", align_bytes=64)
+            return g_r
+
+        def r_lay(g_r, banks, n):
+            nc.vector.tensor_tensor(
+                out=g_r[:, n * P : (n + 1) * P, :], in0=banks[n][:].rearrange("p t c -> p c t"),
+                in1=ab[:].unsqueeze(1).to_broadcast([P, P, 4]), op=ALU.add,
+            )
+
+        def r_quant(th, g_r):
+            quant(
+                g_r[:].rearrange("p c t -> p (c t)"),
+                rc[:, th * HALF : (th + 1) * HALF], rs[:, th * HALF : (th + 1) * HALF],
+            )
+
+        def gating512(th, i):
             tok = slice(th * HALF, (th + 1) * HALF)
-            h_t = gwork.tile([P, 2, HALF], F32, tag="h")
-            e_t = gwork.tile([P, 2, HALF], F32, tag="e")
+            banks = []
             for e in range(2):
-                d = 2 * i + e
-                p2 = psum.tile([P, HALF], F32, name="p2_%d" % e, tag="bank")
+                p2 = psum.tile([P, HALF], F32, name="p2", tag="bank")
                 a = (i * 4 + 3) * 256 + e * P
                 mx(p2[:], wc[:, a : a + P], ws[:, a : a + P], rc[:, tok], rs[:, tok], True, True)
-                p3 = psum.tile([P, HALF], F32, name="p3_%d" % e, tag="bank")
+                p3 = psum.tile([P, HALF], F32, name="p3", tag="bank")
                 for s in range(3):
                     a = (i * 4 + s) * 256 + e * P
                     b = (th * 3 + s) * HALF
                     mx(p3[:], wc[:, a : a + P], ws[:, a : a + P], gc[:, b : b + HALF], gs[:, b : b + HALF], s == 0, s == 2)
-                nc.scalar.activation(out=h_t[:, e, :], in_=p3[:], func=ACT.Sigmoid, bias=ngb[:, d : d + 1], scale=-1.0)
-                nc.vector.scalar_tensor_tensor(
-                    out=e_t[:, e, :], in0=p2[:], scalar=ob[:, d : d + 1], in1=gx5[:, th, i // 2, :, 2 * (i % 2) + e],
-                    op0=ALU.add, op1=ALU.subtract,
-                )
-            nc.vector.tensor_tensor(out=m_t[:, 2 * i : 2 * i + 2, :], in0=h_t[:], in1=e_t[:], op=ALU.mult)
+                banks.append((p2, p3))
+            return banks
 
-        with ExitStack() as front:
-            actraw = front.enter_context(tc.tile_pool(name="actraw", bufs=5))
-            wraw = front.enter_context(tc.tile_pool(name="wraw", bufs=4))
-            grp = front.enter_context(tc.tile_pool(name="grp", bufs=3))
-            grpw = front.enter_context(tc.tile_pool(name="grpw", bufs=2))
-            rpool = front.enter_context(tc.tile_pool(name="rpool", bufs=2))
+        def sig512(i, e, banks):
+            d = 2 * i + e
+            h_t = gwork.tile([P, HALF], F32, name="h_t", tag="h")
+            nc.scalar.activation(out=h_t[:], in_=banks[e][1][:], func=ACT.Sigmoid, bias=ngb[:, d : d + 1], scale=-1.0)
+            return h_t
 
-            nc.sync.dma_start(out=vec[8:10, :], in_=attn_out_b.rearrange("(r c) -> r c", c=256))
-            nc.sync.dma_start(out=vec[0:4, :], in_=gate_b.rearrange("(r c) -> r c", c=256))
-            nc.sync.dma_start(out=vec[4:8, :], in_=op_b.rearrange("(r c) -> r c", c=256))
+        def diff512(th, i, e, banks):
+            d = 2 * i + e
+            e_t = gwork.tile([P, HALF], F32, name="e_t", tag="e")
+            nc.vector.scalar_tensor_tensor(
+                out=e_t[:], in0=banks[e][0][:], scalar=ob[:, d : d + 1], in1=gx5[:, th, i // 2, :, 2 * (i % 2) + e],
+                op0=ALU.add, op1=ALU.subtract,
+            )
+            return e_t
 
-            x_raw = keep.tile([P, 4, 2 * D], BF16)
-            c_raw = []
-            q_raw = []
-            gw_raw = []
-            ow_raw = []
+        def mul512(th, i, e, h_t, e_t):
+            nc.gpsimd.tensor_tensor(out=m_half[th][:, 2 * i + e, :], in0=h_t[:], in1=e_t[:], op=ALU.mult)
 
-            def load_act(src, th, nm):
-                t = actraw.tile([P, 2, 2 * M], BF16, name=nm, tag="act")
-                nc.sync.dma_start(out=t[:], in_=src[:, 2 * th : 2 * th + 2, :])
-                return t
-
-            c_raw.append(load_act(c_d, 0, "c_raw0"))
-            aw_raw = load_act(aw_d, 0, "aw_raw")
-            c_raw.append(load_act(c_d, 1, "c_raw1"))
-            nc.sync.dma_start(out=x_raw[:, 0:2, :], in_=x_d[:, 0:2, :])
-            q_raw.append(load_act(q_d, 0, "q_raw0"))
-            for i in range(4):
-                g_t = wraw.tile([P, 2 * (D + M)], BF16, name="gw_raw%d" % i, tag="gwraw")
-                nc.sync.dma_start(out=g_t[:], in_=gw_d[:, i, :])
-                gw_raw.append(g_t)
-                o_t = wraw.tile([P, 2 * M], BF16, name="ow_raw%d" % i, tag="owraw")
-                nc.sync.dma_start(out=o_t[:], in_=ow_d[:, i, :])
-                ow_raw.append(o_t)
-            nc.sync.dma_start(out=x_raw[:, 2:4, :], in_=x_d[:, 2:4, :])
-            q_raw.append(load_act(q_d, 1, "q_raw1"))
-            lg_bc = keep.tile([P, D], BF16)
-            nc.sync.dma_start(out=lg_bc[:], in_=ln_g.partition_broadcast(P))
-            lb_bc = keep.tile([P, D], BF16)
-            nc.sync.dma_start(out=lb_bc[:], in_=ln_b.partition_broadcast(P))
-
-            def front_small(raw_t, codes, scales, engs):
-                g = grp.tile([P, 4 * HALF], BF16, tag="ga", align_bytes=64)
-                w = words(raw_t)
-                for il in range(2):
-                    bank(w, il * M, M // 2, g[:, il * 1024 : (il + 1) * 1024], engs[il])
-                quant(g[:], codes, scales)
-
-            def front_x(th, engs):
-                w = words(x_raw)
-                n = 0
-                for g in range(2):
-                    for il in range(2):
-                        a = ((th * 2 + g) * HALF + il * 256) * 4
-                        bank(w, (2 * th + il) * D + g * 256, D // 2, gx[:, a : a + 1024], engs[n])
-                        n += 1
-                quant(
-                    gx[:, th * 4096 : (th + 1) * 4096],
-                    gc[:, th * 1536 : th * 1536 + 1024],
-                    gs[:, th * 1536 : th * 1536 + 1024],
-                )
-
-            def front_w(i, engs):
-                g = grpw.tile([P, 4 * 4 * 256], BF16, tag="gw", align_bytes=64)
-                gww = gw_raw[i][:].bitcast(F32)
+        def gating256(quarter, i):
+            th, ql = quarter // 2, quarter % 2
+            tok = slice(quarter * 256, (quarter + 1) * 256)
+            p2 = psum.tile([P, 2, 256], F32, name="p2q", tag="bank")
+            p3 = psum.tile([P, 2, 256], F32, name="p3q", tag="bank")
+            for e in range(2):
+                a = (i * 4 + 3) * 256 + e * P
+                mx(p2[:, e, :], wc[:, a : a + P], ws[:, a : a + P], rc[:, tok], rs[:, tok], True, True)
+            for e in range(2):
                 for s in range(3):
-                    bank(gww, s * 256, (D + M) // 2, g[:, s * 1024 : (s + 1) * 1024], engs[s])
-                bank(ow_raw[i][:].bitcast(F32), 0, M // 2, g[:, 3072:4096], engs[3])
-                quant(g[:], wc[:, i * 1024 : (i + 1) * 1024], ws[:, i * 1024 : (i + 1) * 1024])
+                    a = (i * 4 + s) * 256 + e * P
+                    b = (th * 3 + s) * HALF + ql * 256
+                    mx(p3[:, e, :], wc[:, a : a + P], ws[:, a : a + P], gc[:, b : b + 256], gs[:, b : b + 256], s == 0, s == 2)
+            return p2, p3
 
-            def mm1(th):
-                r_t = rpool.tile([P, 4, HALF], BF16, tag="rT")
-                for t in range(4):
-                    p1 = psum.tile([P, HALF], F32, name="p1_%d_%d" % (th, t), tag="bank")
-                    mx(
-                        p1[:], wa[:, t * P : (t + 1) * P], was[:, t * P : (t + 1) * P],
-                        cc[:, th * HALF : (th + 1) * HALF], cs[:, th * HALF : (th + 1) * HALF], True, True,
-                    )
-                    nc.scalar.activation(out=r_t[:, t, :], in_=p1[:], func=ACT.Identity, bias=ab[:, t : t + 1], scale=1.0)
-                g_r = rpool.tile([P, HALF, 4], BF16, tag="gr", align_bytes=64)
-                nc.vector.tensor_copy(
-                    out=g_r[:].rearrange("p (c i) t -> p c t i", i=4), in_=r_t[:].rearrange("p t (c i) -> p c t i", i=4)
+        def blend256(quarter, i, banks, eng):
+            th, ql = quarter // 2, quarter % 2
+            p2, p3 = banks
+            cols = slice(ql * 256, (ql + 1) * 256)
+            h_t = gwork.tile([P, 2, 256], F32, name="h_t", tag="h")
+            e_t = gwork.tile([P, 2, 256], F32, name="e_t", tag="e")
+            for e in range(2):
+                d = 2 * i + e
+                nc.scalar.activation(out=h_t[:, e, :], in_=p3[:, e, :], func=ACT.Sigmoid, bias=ngb[:, d : d + 1], scale=-1.0)
+                nc.vector.scalar_tensor_tensor(
+                    out=e_t[:, e, :], in0=p2[:, e, :], scalar=ob[:, d : d + 1],
+                    in1=gx5[:, th, i // 2, cols, 2 * (i % 2) + e], op0=ALU.add, op1=ALU.subtract,
                 )
-                quant(
-                    g_r[:].rearrange("p c t -> p (c t)"),
-                    rc[:, th * HALF : (th + 1) * HALF], rs[:, th * HALF : (th + 1) * HALF],
-                )
+            eng.tensor_tensor(out=m_half[th][:, 2 * i : 2 * i + 2, cols], in0=h_t[:], in1=e_t[:], op=ALU.mult)
 
-            front_small(c_raw[0], cc[:, 0:HALF], cs[:, 0:HALF], "sv")
-            front_small(aw_raw, wa[:], was[:], "sv")
-
-            vt = psum.tile([P, 2, 256], F32, tag="bank")
-            nc.tensor.transpose(vt[:, 0, 0:P], vec[:].bitcast(F32), ident_f[:])
-            vt_b = vt[:, 0, 0:16].bitcast(BF16)
-            ngb = keep.tile([P, 8], F32)
-            nc.vector.tensor_scalar_mul(out=ngb[:], in0=vt_b[:, 0:8], scalar1=-1.0)
-            ob = keep.tile([P, 8], F32)
-            nc.vector.tensor_copy(out=ob[:], in_=vt_b[:, 8:16])
-            ab = keep.tile([P, 4], F32)
-            nc.vector.tensor_copy(out=ab[:], in_=vt_b[:, 16:20])
-
-            mm1(0)
-            front_small(c_raw[1], cc[:, HALF:T], cs[:, HALF:T], "sv")
-            mm1(1)
-            front_x(0, "svsv")
-            front_small(q_raw[0], gc[:, 1024:1536], gs[:, 1024:1536], "sv")
-            front_w(0, "ssss")
-            front_w(1, "ssss")
-            for i in range(4):
-                gating(0, i, m0)
-                if i < 2:
-                    front_w(i + 2, "ssss")
-                if i == 2:
-                    front_x(1, "ssss")
-                if i == 3:
-                    front_small(q_raw[1], gc[:, 1536 + 1024 : 3072], gs[:, 1536 + 1024 : 3072], "ss")
-
-        late = stack.enter_context(tc.tile_pool(name="late", bufs=1))
-        lny = stack.enter_context(tc.tile_pool(name="lny", bufs=4))
-        lnw = stack.enter_context(tc.tile_pool(name="lnw", bufs=8))
-        small8 = stack.enter_context(tc.tile_pool(name="small8", bufs=8))
-        m1 = late.tile([P, 8, HALF], F32)
-        lg32 = late.tile([P, D], BF16)
-        nc.vector.tensor_scalar_mul(out=lg32[:], in0=lg_bc[:], scalar1=32.0)
-
-        def layernorm(th, j, m_t, on_vector):
-            i_tok = 2 * th + j // 2
-            e_tok = j % 2
+        def y_tile(k):
+            th, j = k // 4, k % 4
             banks = []
             for g in range(2):
-                yp = psum.tile([P, 2, 256], F32, name="yp%d" % g, tag="bank")
+                yp = psum.tile([P, 2, 256], F32, name="yp", tag="bank")
                 banks.append(yp)
+                o = (k % 2) * D + g * 512
                 nc.tensor.matmul(
-                    out=yp[:], lhsT=ident_b[:],
-                    rhs=x_raw[:, i_tok, e_tok * D + g * 512 : e_tok * D + (g + 1) * 512].rearrange("p (a e) -> p e a", e=2),
+                    out=yp[:], lhsT=ident_b[:], rhs=x_raw[:, k // 2, o : o + 512].rearrange("p (a e) -> p e a", e=2),
                     start=True, stop=False,
                 )
                 for e in range(2):
                     for u in range(2):
                         nc.tensor.matmul(
-                            out=yp[:, e, u * P : (u + 1) * P], lhsT=m_t[:, 2 * (2 * g + u) + e, j * P : (j + 1) * P],
+                            out=yp[:, e, u * P : (u + 1) * P], lhsT=m_half[th][:, 2 * (2 * g + u) + e, j * P : (j + 1) * P],
                             rhs=ident_f[:], is_transpose=True, start=False, stop=(e == 1 and u == 1),
                         )
-            nmean = small.tile([P, 1], F32, tag="nmean")
-            ve = small.tile([P, 1], F32, tag="ve")
-            if on_vector:
-                stats = small.tile([P, 2, 6], F32, tag="stats")
-                for g in range(2):
-                    nc.vector.bn_stats(out=stats[:, g, :], in_=banks[g][:].rearrange("p e a -> p (e a)"))
-                mv = small.tile([P, 2], F32, tag="mv")
-                nc.vector.bn_aggr(out=mv[:], in_=stats[:].rearrange("p g s -> p (g s)"))
-                nc.vector.tensor_scalar_mul(out=nmean[:], in0=mv[:, 0:1], scalar1=-1.0)
-                nc.vector.tensor_scalar(
-                    out=ve[:], in0=mv[:, 1:2], scalar1=1.0 * D, scalar2=D * LN_EPS, op0=ALU.mult, op1=ALU.add
-                )
-            else:
-                y_t = lny.tile([P, D], F32, tag="y")
-                s1 = small.tile([P, 2], F32, tag="s1")
-                for g in range(2):
-                    nc.scalar.activation(
-                        out=y_t[:, g * 512 : (g + 1) * 512], in_=banks[g][:].rearrange("p e a -> p (e a)"),
-                        func=ACT.Identity, scale=-1.0 / D, accum_out=s1[:, g : g + 1],
-                    )
-                nc.scalar.activation(out=nmean[:], in_=s1[:, 0:1], func=ACT.Identity, bias=s1[:, 1:2], scale=1.0)
-                junk = late.tile([P, D], BF16, tag="junk")
-                s2 = small.tile([P, 1], F32, tag="s2")
+            return banks
+
+        def stats_v(banks):
+            stats = small.tile([P, 2, 6], F32, name="stats", tag="stats")
+            for g in range(2):
+                nc.vector.bn_stats(out=stats[:, g, :], in_=banks[g][:].rearrange("p e a -> p (e a)"))
+            mv = small.tile([P, 2], F32, name="mv", tag="mv")
+            nc.vector.bn_aggr(out=mv[:], in_=stats[:].rearrange("p g s -> p (g s)"))
+            ve = small.tile([P, 1], F32, name="ve", tag="ve")
+            nc.gpsimd.tensor_scalar(out=ve[:], in0=mv[:, 1:2], scalar1=1.0, scalar2=LN_EPS, op0=ALU.mult, op1=ALU.add)
+            rstd = small.tile([P, 1], F32, name="rstd", tag="rstd")
+            nc.gpsimd.tensor_tensor(out=rstd[:], in0=ve[:], in1=mhalf[:], op=ALU.pow)
+            nmean = small.tile([P, 1], F32, name="nmean", tag="nmean")
+            nc.vector.tensor_scalar_mul(out=nmean[:], in0=mv[:, 0:1], scalar1=-1.0)
+            return nmean, rstd
+
+        def stats_s(banks):
+            y_t = aux.tile([P, D], F32, name="y_t", tag="y")
+            s1 = small.tile([P, 2], F32, name="s1", tag="s1")
+            for g in range(2):
                 nc.scalar.activation(
-                    out=junk[:], in_=y_t[:], func=ACT.Square, bias=nmean[:], scale=-1.0 * D, accum_out=s2[:]
+                    out=y_t[:, g * 512 : (g + 1) * 512], in_=banks[g][:].rearrange("p e a -> p (e a)"),
+                    func=ACT.Identity, scale=-1.0 / D, accum_out=s1[:, g : g + 1],
                 )
-                nc.scalar.add(out=ve[:], in_=s2[:], add=D * LN_EPS)
-            w_t = lnw.tile([P, D], F32, tag="w")
+            nmean = small.tile([P, 1], F32, name="nmean", tag="nmean")
+            nc.scalar.activation(out=nmean[:], in_=s1[:, 0:1], func=ACT.Identity, bias=s1[:, 1:2], scale=1.0)
+            junk = aux.tile([P, D], BF16, name="junk", tag="junk")
+            s2 = small.tile([P, 1], F32, name="s2", tag="s2")
+            nc.scalar.activation(
+                out=junk[:], in_=y_t[:], func=ACT.Square, bias=nmean[:], scale=-1.0 * D, accum_out=s2[:]
+            )
+            ve = small.tile([P, 1], F32, name="ve", tag="ve")
+            nc.gpsimd.tensor_scalar(out=ve[:], in0=s2[:], scalar1=1.0 / D, scalar2=LN_EPS, op0=ALU.mult, op1=ALU.add)
+            rstd = small.tile([P, 1], F32, name="rstd", tag="rstd")
+            nc.gpsimd.tensor_tensor(out=rstd[:], in0=ve[:], in1=mhalf[:], op=ALU.pow)
+            return nmean, rstd
+
+        def scale(banks, nmean):
+            w_t = lnw.tile([P, D], F32, name="w_t", tag="w")
             for g in range(2):
                 nc.vector.scalar_tensor_tensor(
                     out=w_t[:, g * 512 : (g + 1) * 512].rearrange("p (a e) -> p a e", e=2),
                     in0=banks[g][:].rearrange("p e a -> p a e"), scalar=nmean[:],
-                    in1=lg32[:, g * 512 : (g + 1) * 512].rearrange("p (a e) -> p a e", e=2),
+                    in1=lg_bc[:, g * 512 : (g + 1) * 512].rearrange("p (a e) -> p a e", e=2),
                     op0=ALU.add, op1=ALU.mult,
                 )
-            rs32 = small8.tile([P, 1], F32, tag="rs32")
-            nc.gpsimd.tensor_tensor(out=rs32[:], in0=ve[:], in1=mhalf[:], op=ALU.pow)
-            return w_t, rs32
+            return w_t
 
-        def layernorm_out(th, j, w_t, rs32):
-            i_tok = 2 * th + j // 2
-            e_tok = j % 2
-            o_t = lny.tile([P, D], F32, tag="o")
-            pieces = 2 if (th == 1 and j == 3) else 1
+        def finish(k, w_t, rstd, how):
+            if how == "g":
+                nc.scalar.activation(out=w_t[:], in_=w_t[:], func=ACT.Copy, scale=rstd[:])
+                nc.gpsimd.tensor_tensor(out=w_t[:], in0=w_t[:], in1=lb_bc[:], op=ALU.add)
+                nc.sync.dma_start(out=out_d[:, k // 2, k % 2, :], in_=w_t[:])
+                return
+            pieces = 2 if how == "vv" else 1
             width = D // pieces
             for c in range(pieces):
                 cols = slice(c * width, (c + 1) * width)
                 nc.vector.scalar_tensor_tensor(
-                    out=o_t[:, cols], in0=w_t[:, cols], scalar=rs32[:], in1=lb_bc[:, cols], op0=ALU.mult, op1=ALU.add
+                    out=w_t[:, cols], in0=w_t[:, cols], scalar=rstd[:], in1=lb_bc[:, cols], op0=ALU.mult, op1=ALU.add
                 )
-                nc.sync.dma_start(out=out_d[:, i_tok, e_tok, cols], in_=o_t[:, cols])
+                nc.sync.dma_start(out=out_d[:, k // 2, k % 2, cols], in_=w_t[:, cols])
 
-        pending = []
+        t_c0 = small_turn(c_raw0)
+        t_aw = small_turn(aw_raw)
+        vt = psum.tile([P, 2, 256], F32, name="vt", tag="bank")
+        nc.tensor.transpose(vt[:, 0, 0:P], vec[:].bitcast(F32), ident_f[:])
+        g_c0 = small_lay(t_c0, "sv")
+        g_aw = small_lay(t_aw, "sv")
+        quant(g_c0[:], cc[:, 0:HALF], cs[:, 0:HALF])
+        quant(g_aw[:], wa[:], was[:])
+        vt_b = vt[:, 0, 0:16].bitcast(BF16)
+        ab = keep.tile([P, 4], F32)
+        nc.vector.tensor_copy(out=ab[:], in_=vt_b[:, 16:20])
+        ngb = keep.tile([P, 8], F32)
+        nc.vector.tensor_scalar_mul(out=ngb[:], in0=vt_b[:, 0:8], scalar1=-1.0)
+        ob = keep.tile([P, 8], F32)
+        nc.vector.tensor_copy(out=ob[:], in_=vt_b[:, 8:16])
+
+        t_xa = x_turn(0, 0)
+        t_xb = x_turn(0, 1)
+        b_r = mm1(0)
+        x_lay(0, 0, t_xa, "ss")
+        x_lay(0, 1, t_xb, "ss")
+        g_r = r_tile()
+        r_lay(g_r, b_r, 0)
+        x_quant(0, 0)
+        for n in range(1, 4):
+            r_lay(g_r, b_r, n)
+        t_q0 = small_turn(q_raw0)
+        g_q0 = small_lay(t_q0, "ss")
+        x_quant(0, 1)
+        r_quant(0, g_r)
+        t_w = w_turn(0)
+        g_w = w_tile()
+        w_lay(g_w, t_w, 0, "s")
+        w_lay(g_w, t_w, 1, "s")
+        w_lay(g_w, t_w, 2, "s")
+        q_quant(0, g_q0)
+        w_lay(g_w, t_w, 3, "s")
+        w_quant(0, g_w, 0)
+        w_quant(0, g_w, 1)
+        t_w = w_turn(1)
+
         for i in range(4):
-            gating(1, i, m1)
-            pending.append((0, i) + layernorm(0, i, m0, False))
-        for j in range(4):
-            pending.append((1, j) + layernorm(1, j, m1, j == 3))
-        for th, j, w_t, rs32 in pending:
-            layernorm_out(th, j, w_t, rs32)
+            banks = gating512(0, i)
+            if i == 0:
+                t_c1 = small_turn(c_raw1)
+            if i == 2:
+                t_xa = x_turn(1, 0)
+                t_xb = x_turn(1, 1)
+            if i == 3:
+                t_q1 = small_turn(q_raw1)
+            if i < 2:
+                t_w2 = w_turn(i + 2)
+            if i < 3:
+                g_w = w_tile()
+                for s in range(3):
+                    w_lay(g_w, t_w, s, "s")
+                w_lay(g_w, t_w, 3, "s")
+            e0 = diff512(0, i, 0, banks)
+            h0 = sig512(i, 0, banks)
+            mul512(0, i, 0, h0, e0)
+            if i < 3:
+                w_quant(i + 1, g_w, 0)
+            e1 = diff512(0, i, 1, banks)
+            h1 = sig512(i, 1, banks)
+            mul512(0, i, 1, h1, e1)
+            if i < 3:
+                w_quant(i + 1, g_w, 1)
+            if i < 2:
+                t_w = t_w2
+            if i == 0:
+                g_c1 = small_lay(t_c1, "sv")
+                quant(g_c1[:], cc[:, HALF:T], cs[:, HALF:T])
+            if i == 1:
+                b_r = mm1(1)
+                g_r = r_tile()
+                for n in range(4):
+                    r_lay(g_r, b_r, n)
+            if i == 2:
+                r_quant(1, g_r)
+                x_lay(1, 0, t_xa, "ss")
+                x_lay(1, 1, t_xb, "ss")
+                x_quant(1, 0)
+            if i == 3:
+                x_quant(1, 1)
+                g_q1 = small_lay(t_q1, "sv")
+                q_quant(1, g_q1)
+
+        plan = [
+            (0, "s", "v"), (1, "s", "v"), (2, "s", "v"), (3, "s", "g"), None, (4, "v", "g"), (5, "s", "v"), None, (6, "s", "v"), (7, "v", "vv"),
+        ]
+        to_scale = None
+        to_finish = None
+        for n in range(12):
+            if n < 8:
+                banks = gating256(2 + n // 4, n % 4)
+            if n < 10 and plan[n] is not None:
+                ybanks = y_tile(plan[n][0])
+            if n < 8:
+                blend256(2 + n // 4, n % 4, banks, nc.gpsimd if n < 6 else nc.vector)
+            if to_finish is not None:
+                finish(*to_finish)
+                to_finish = None
+            if to_scale is not None:
+                k, fin, yb, nmean, rstd = to_scale
+                to_finish = (k, scale(yb, nmean), rstd, fin)
+                to_scale = None
+            if n < 10 and plan[n] is not None:
+                k, how, fin = plan[n]
+                nmean, rstd = stats_v(ybanks) if how == "v" else stats_s(ybanks)
+                to_scale = (k, fin, ybanks, nmean, rstd)

@@ -67,8 +67,12 @@ def tile_rotelearningmemory_pa_kernel(
         x_raw = keep.tile([P, 4, 2 * D], BF16)
         lg_bc = keep.tile([P, D], BF16)
         lb_bc = keep.tile([P, D], BF16)
+        lbz = keep.tile([P, D], BF16)
 
         nc.vector.memset(vec[:].bitcast(F32), 0.0)
+        nc.gpsimd.memset(lbz[:].bitcast(F32), 0.0)
+        ones = keep.tile([P, P], BF16)
+        nc.gpsimd.memset(ones[:], 1.0)
         ident_f = keep.tile([P, P], F32)
         make_identity(nc, ident_f[:])
         ident_b = keep.tile([P, P], BF16)
@@ -80,9 +84,11 @@ def tile_rotelearningmemory_pa_kernel(
         warm_out = keep.tile([P, 1], F32)
         nc.scalar.activation(out=warm_out[:], in_=warm_in[:], func=ACT.Sigmoid)
 
-        def load_act(src, th, nm):
+        def load_act(src, th, nm, parts):
             t = wraw.tile([P, 2, 2 * M], BF16, name=nm, tag="act")
-            nc.sync.dma_start(out=t[:], in_=src[:, 2 * th : 2 * th + 2, :])
+            n = 2 // parts
+            for j in range(parts):
+                nc.sync.dma_start(out=t[:, j * n : (j + 1) * n, :], in_=src[:, 2 * th + j * n : 2 * th + (j + 1) * n, :])
             return t
 
         def load_w(i):
@@ -92,19 +98,22 @@ def tile_rotelearningmemory_pa_kernel(
             nc.sync.dma_start(out=o_t[:], in_=ow_d[:, i, :])
             return g_t, o_t
 
-        c_raw0 = load_act(c_d, 0, "c_raw0")
+        c_raw0 = load_act(c_d, 0, "c_raw0", 2)
+        aw_raw = load_act(aw_d, 0, "aw_raw", 2)
+        nc.sync.dma_start(out=x_raw[:, 0, :], in_=x_d[:, 0, :])
         nc.sync.dma_start(out=vec[8:10, :], in_=attn_out_b.rearrange("(r c) -> r c", c=256))
         nc.sync.dma_start(out=vec[0:4, :], in_=gate_b.rearrange("(r c) -> r c", c=256))
         nc.sync.dma_start(out=vec[4:8, :], in_=op_b.rearrange("(r c) -> r c", c=256))
-        aw_raw = load_act(aw_d, 0, "aw_raw")
-        nc.sync.dma_start(out=x_raw[:, 0:2, :], in_=x_d[:, 0:2, :])
-        q_raw0 = load_act(q_d, 0, "q_raw0")
-        w_raw = [load_w(i) for i in range(2)]
-        c_raw1 = load_act(c_d, 1, "c_raw1")
+        w_raw = [load_w(0)]
+        nc.sync.dma_start(out=x_raw[:, 1, :], in_=x_d[:, 1, :])
+        q_raw0 = load_act(q_d, 0, "q_raw0", 1)
+        w_raw.append(load_w(1))
+        c_raw1 = load_act(c_d, 1, "c_raw1", 1)
         w_raw += [load_w(i) for i in range(2, 4)]
         nc.sync.dma_start(out=x_raw[:, 2:4, :], in_=x_d[:, 2:4, :])
-        q_raw1 = load_act(q_d, 1, "q_raw1")
+        q_raw1 = load_act(q_d, 1, "q_raw1", 1)
         nc.sync.dma_start(out=lg_bc[:], in_=ln_g.partition_broadcast(P))
+        nc.sync.dma_start(out=lbz[0:1, :], in_=ln_b.rearrange("(o d) -> o d", o=1))
         nc.sync.dma_start(out=lb_bc[:], in_=ln_b.partition_broadcast(P))
 
         def turn(words, base, row_words):
@@ -145,14 +154,14 @@ def tile_rotelearningmemory_pa_kernel(
                 lay(tps[il], g[:, il * 1024 : (il + 1) * 1024], engs[il])
             return g
 
-        def x_turn(th, g):
+        def x_turn(i):
             w = words(x_raw)
-            return [turn(w, (2 * th + il) * D + g * 256, D // 2) for il in range(2)]
+            return [turn(w, i * D + g * 256, D // 2) for g in range(2)]
 
-        def x_lay(th, g, tps, engs):
-            for il in range(2):
-                a = ((th * 2 + g) * HALF + il * 256) * 4
-                lay(tps[il], gx[:, a : a + 1024], engs[il])
+        def x_lay(i, tps, engs):
+            for g in range(2):
+                a = ((i // 2 * 2 + g) * HALF + i % 2 * 256) * 4
+                lay(tps[g], gx[:, a : a + 1024], engs[g])
 
         def x_quant(th, g):
             a = th * 1536 + g * 512
@@ -236,7 +245,9 @@ def tile_rotelearningmemory_pa_kernel(
             return e_t
 
         def mul512(th, i, e, h_t, e_t):
-            nc.gpsimd.tensor_tensor(out=m_half[th][:, 2 * i + e, :], in0=h_t[:], in1=e_t[:], op=ALU.mult)
+            for j in range(2):
+                c = slice(j * 256, (j + 1) * 256)
+                nc.gpsimd.tensor_tensor(out=m_half[th][:, 2 * i + e, c], in0=h_t[:, c], in1=e_t[:, c], op=ALU.mult)
 
         def gating256(quarter, i):
             th, ql = quarter // 2, quarter % 2
@@ -311,7 +322,7 @@ def tile_rotelearningmemory_pa_kernel(
                 )
             nmean = small.tile([P, 1], F32, name="nmean", tag="nmean")
             nc.scalar.activation(out=nmean[:], in_=s1[:, 0:1], func=ACT.Identity, bias=s1[:, 1:2], scale=1.0)
-            junk = aux.tile([P, D], BF16, name="junk", tag="junk")
+            junk = aux.tile([P, D], BF16, name="junk", tag="junk", bufs=1)
             s2 = small.tile([P, 1], F32, name="s2", tag="s2")
             nc.scalar.activation(
                 out=junk[:], in_=y_t[:], func=ACT.Square, bias=nmean[:], scale=-1.0 * D, accum_out=s2[:]
@@ -339,23 +350,25 @@ def tile_rotelearningmemory_pa_kernel(
                 nc.gpsimd.tensor_tensor(out=w_t[:], in0=w_t[:], in1=lb_bc[:], op=ALU.add)
                 nc.sync.dma_start(out=out_d[:, k // 2, k % 2, :], in_=w_t[:])
                 return
-            pieces = 2 if how == "vv" else 1
-            width = D // pieces
-            for c in range(pieces):
-                cols = slice(c * width, (c + 1) * width)
+            for g in range(2):
+                cols = slice(g * 512, (g + 1) * 512)
                 nc.vector.scalar_tensor_tensor(
-                    out=w_t[:, cols], in0=w_t[:, cols], scalar=rstd[:], in1=lb_bc[:, cols], op0=ALU.mult, op1=ALU.add
+                    out=w_t[:, cols], in0=w_t[:, cols], scalar=rstd[:], in1=lbp[g][:], op0=ALU.mult, op1=ALU.add
                 )
-                nc.sync.dma_start(out=out_d[:, k // 2, k % 2, cols], in_=w_t[:, cols])
+                if how == "vv":
+                    nc.sync.dma_start(out=out_d[:, k // 2, k % 2, cols], in_=w_t[:, cols])
+            if how != "vv":
+                nc.sync.dma_start(out=out_d[:, k // 2, k % 2, :], in_=w_t[:])
 
         t_c0 = small_turn(c_raw0)
         t_aw = small_turn(aw_raw)
-        vt = psum.tile([P, 2, 256], F32, name="vt", tag="bank")
-        nc.tensor.transpose(vt[:, 0, 0:P], vec[:].bitcast(F32), ident_f[:])
         g_c0 = small_lay(t_c0, "sv")
         g_aw = small_lay(t_aw, "sv")
         quant(g_c0[:], cc[:, 0:HALF], cs[:, 0:HALF])
         quant(g_aw[:], wa[:], was[:])
+        t_xa = x_turn(0)
+        vt = psum.tile([P, 2, 256], F32, name="vt", tag="bank")
+        nc.tensor.transpose(vt[:, 0, 0:P], vec[:].bitcast(F32), ident_f[:])
         vt_b = vt[:, 0, 0:16].bitcast(BF16)
         ab = keep.tile([P, 4], F32)
         nc.vector.tensor_copy(out=ab[:], in_=vt_b[:, 16:20])
@@ -363,30 +376,27 @@ def tile_rotelearningmemory_pa_kernel(
         nc.vector.tensor_scalar_mul(out=ngb[:], in0=vt_b[:, 0:8], scalar1=-1.0)
         ob = keep.tile([P, 8], F32)
         nc.vector.tensor_copy(out=ob[:], in_=vt_b[:, 8:16])
-
-        t_xa = x_turn(0, 0)
-        t_xb = x_turn(0, 1)
         b_r = mm1(0)
-        x_lay(0, 0, t_xa, "ss")
-        x_lay(0, 1, t_xb, "ss")
+        x_lay(0, t_xa, "ss")
         g_r = r_tile()
         r_lay(g_r, b_r, 0)
-        x_quant(0, 0)
-        for n in range(1, 4):
-            r_lay(g_r, b_r, n)
-        t_q0 = small_turn(q_raw0)
-        g_q0 = small_lay(t_q0, "ss")
-        x_quant(0, 1)
-        r_quant(0, g_r)
+        r_lay(g_r, b_r, 1)
         t_w = w_turn(0)
+        r_lay(g_r, b_r, 2)
+        r_lay(g_r, b_r, 3)
         g_w = w_tile()
-        w_lay(g_w, t_w, 0, "s")
-        w_lay(g_w, t_w, 1, "s")
-        w_lay(g_w, t_w, 2, "s")
-        q_quant(0, g_q0)
-        w_lay(g_w, t_w, 3, "s")
+        for s in range(4):
+            w_lay(g_w, t_w, s, "s")
+        t_xb = x_turn(1)
+        t_q0 = small_turn(q_raw0)
+        r_quant(0, g_r)
+        x_lay(1, t_xb, "ss")
         w_quant(0, g_w, 0)
         w_quant(0, g_w, 1)
+        x_quant(0, 0)
+        x_quant(0, 1)
+        g_q0 = small_lay(t_q0, "ss")
+        q_quant(0, g_q0)
         t_w = w_turn(1)
 
         for i in range(4):
@@ -394,8 +404,8 @@ def tile_rotelearningmemory_pa_kernel(
             if i == 0:
                 t_c1 = small_turn(c_raw1)
             if i == 2:
-                t_xa = x_turn(1, 0)
-                t_xb = x_turn(1, 1)
+                t_xa = x_turn(2)
+                t_xb = x_turn(3)
             if i == 3:
                 t_q1 = small_turn(q_raw1)
             if i < 2:
@@ -427,17 +437,21 @@ def tile_rotelearningmemory_pa_kernel(
                     r_lay(g_r, b_r, n)
             if i == 2:
                 r_quant(1, g_r)
-                x_lay(1, 0, t_xa, "ss")
-                x_lay(1, 1, t_xb, "ss")
+                x_lay(2, t_xa, "ss")
+                x_lay(3, t_xb, "ss")
                 x_quant(1, 0)
             if i == 3:
                 x_quant(1, 1)
-                g_q1 = small_lay(t_q1, "sv")
+                g_q1 = small_lay(t_q1, "ss")
                 q_quant(1, g_q1)
 
-        plan = [
-            (0, "s", "v"), (1, "s", "v"), (2, "s", "v"), (3, "s", "g"), None, (4, "v", "g"), (5, "s", "v"), None, (6, "s", "v"), (7, "v", "vv"),
-        ]
+        lbp = []
+        for g in range(2):
+            lb_t = psum.tile([P, HALF], F32, name="lb_t", tag="bank")
+            nc.tensor.matmul(out=lb_t[:], lhsT=ones[:], rhs=lbz[:, g * 512 : (g + 1) * 512], start=True, stop=True)
+            lbp.append(lb_t)
+
+        plan = [(0, "s", "v"), (1, "v", "g"), (2, "s", "g"), (3, "s", "v"), None, (4, "v", "g"), (5, "s", "v"), None, (6, "s", "v"), (7, "s", "vv")]
         to_scale = None
         to_finish = None
         for n in range(12):

@@ -67,12 +67,8 @@ def tile_rotelearningmemory_pa_kernel(
         x_raw = keep.tile([P, 4, 2 * D], BF16)
         lg_bc = keep.tile([P, D], BF16)
         lb_bc = keep.tile([P, D], BF16)
-        lbz = keep.tile([P, D], BF16)
 
         nc.vector.memset(vec[:].bitcast(F32), 0.0)
-        nc.gpsimd.memset(lbz[:].bitcast(F32), 0.0)
-        ones = keep.tile([P, P], BF16)
-        nc.gpsimd.memset(ones[:], 1.0)
         ident_f = keep.tile([P, P], F32)
         make_identity(nc, ident_f[:])
         ident_b = keep.tile([P, P], BF16)
@@ -113,7 +109,6 @@ def tile_rotelearningmemory_pa_kernel(
         nc.sync.dma_start(out=x_raw[:, 2:4, :], in_=x_d[:, 2:4, :])
         q_raw1 = load_act(q_d, 1, "q_raw1", 1)
         nc.sync.dma_start(out=lg_bc[:], in_=ln_g.partition_broadcast(P))
-        nc.sync.dma_start(out=lbz[0:1, :], in_=ln_b.rearrange("(o d) -> o d", o=1))
         nc.sync.dma_start(out=lb_bc[:], in_=ln_b.partition_broadcast(P))
 
         def turn(words, base, row_words):
@@ -298,21 +293,22 @@ def tile_rotelearningmemory_pa_kernel(
                         )
             return banks
 
+        def rstd_of(var, scl):
+            ve = small.tile([P, 1], F32, name="ve", tag="ve")
+            nc.gpsimd.tensor_scalar(out=ve[:], in0=var, scalar1=scl, scalar2=LN_EPS, op0=ALU.mult, op1=ALU.add)
+            rstd = small.tile([P, 1], F32, name="rstd", tag="rstd")
+            nc.gpsimd.tensor_tensor(out=rstd[:], in0=ve[:], in1=mhalf[:], op=ALU.pow)
+            return rstd
+
         def stats_v(banks):
             stats = small.tile([P, 2, 6], F32, name="stats", tag="stats")
             for g in range(2):
                 nc.vector.bn_stats(out=stats[:, g, :], in_=banks[g][:].rearrange("p e a -> p (e a)"))
             mv = small.tile([P, 2], F32, name="mv", tag="mv")
             nc.vector.bn_aggr(out=mv[:], in_=stats[:].rearrange("p g s -> p (g s)"))
-            ve = small.tile([P, 1], F32, name="ve", tag="ve")
-            nc.gpsimd.tensor_scalar(out=ve[:], in0=mv[:, 1:2], scalar1=1.0, scalar2=LN_EPS, op0=ALU.mult, op1=ALU.add)
-            rstd = small.tile([P, 1], F32, name="rstd", tag="rstd")
-            nc.gpsimd.tensor_tensor(out=rstd[:], in0=ve[:], in1=mhalf[:], op=ALU.pow)
-            nmean = small.tile([P, 1], F32, name="nmean", tag="nmean")
-            nc.vector.tensor_scalar_mul(out=nmean[:], in0=mv[:, 0:1], scalar1=-1.0)
-            return nmean, rstd
+            return mv
 
-        def stats_s(banks):
+        def sums_s(banks):
             y_t = aux.tile([P, D], F32, name="y_t", tag="y")
             s1 = small.tile([P, 2], F32, name="s1", tag="s1")
             for g in range(2):
@@ -320,27 +316,29 @@ def tile_rotelearningmemory_pa_kernel(
                     out=y_t[:, g * 512 : (g + 1) * 512], in_=banks[g][:].rearrange("p e a -> p (e a)"),
                     func=ACT.Identity, scale=-1.0 / D, accum_out=s1[:, g : g + 1],
                 )
+            return y_t, s1
+
+        def nmean_s(s1):
             nmean = small.tile([P, 1], F32, name="nmean", tag="nmean")
             nc.scalar.activation(out=nmean[:], in_=s1[:, 0:1], func=ACT.Identity, bias=s1[:, 1:2], scale=1.0)
+            return nmean
+
+        def squares_s(y_t, nmean):
             junk = aux.tile([P, D], BF16, name="junk", tag="junk", bufs=1)
             s2 = small.tile([P, 1], F32, name="s2", tag="s2")
             nc.scalar.activation(
                 out=junk[:], in_=y_t[:], func=ACT.Square, bias=nmean[:], scale=-1.0 * D, accum_out=s2[:]
             )
-            ve = small.tile([P, 1], F32, name="ve", tag="ve")
-            nc.gpsimd.tensor_scalar(out=ve[:], in0=s2[:], scalar1=1.0 / D, scalar2=LN_EPS, op0=ALU.mult, op1=ALU.add)
-            rstd = small.tile([P, 1], F32, name="rstd", tag="rstd")
-            nc.gpsimd.tensor_tensor(out=rstd[:], in0=ve[:], in1=mhalf[:], op=ALU.pow)
-            return nmean, rstd
+            return s2
 
-        def scale(banks, nmean):
+        def scale(banks, shift, op):
             w_t = lnw.tile([P, D], F32, name="w_t", tag="w")
             for g in range(2):
                 nc.vector.scalar_tensor_tensor(
                     out=w_t[:, g * 512 : (g + 1) * 512].rearrange("p (a e) -> p a e", e=2),
-                    in0=banks[g][:].rearrange("p e a -> p a e"), scalar=nmean[:],
+                    in0=banks[g][:].rearrange("p e a -> p a e"), scalar=shift,
                     in1=lg_bc[:, g * 512 : (g + 1) * 512].rearrange("p (a e) -> p a e", e=2),
-                    op0=ALU.add, op1=ALU.mult,
+                    op0=op, op1=ALU.mult,
                 )
             return w_t
 
@@ -350,15 +348,14 @@ def tile_rotelearningmemory_pa_kernel(
                 nc.gpsimd.tensor_tensor(out=w_t[:], in0=w_t[:], in1=lb_bc[:], op=ALU.add)
                 nc.sync.dma_start(out=out_d[:, k // 2, k % 2, :], in_=w_t[:])
                 return
-            for g in range(2):
-                cols = slice(g * 512, (g + 1) * 512)
+            pieces = 2 if how == "vv" else 1
+            width = D // pieces
+            for c in range(pieces):
+                cols = slice(c * width, (c + 1) * width)
                 nc.vector.scalar_tensor_tensor(
-                    out=w_t[:, cols], in0=w_t[:, cols], scalar=rstd[:], in1=lbp[g][:], op0=ALU.mult, op1=ALU.add
+                    out=w_t[:, cols], in0=w_t[:, cols], scalar=rstd[:], in1=lb_bc[:, cols], op0=ALU.mult, op1=ALU.add
                 )
-                if how == "vv":
-                    nc.sync.dma_start(out=out_d[:, k // 2, k % 2, cols], in_=w_t[:, cols])
-            if how != "vv":
-                nc.sync.dma_start(out=out_d[:, k // 2, k % 2, :], in_=w_t[:])
+                nc.sync.dma_start(out=out_d[:, k // 2, k % 2, cols], in_=w_t[:, cols])
 
         t_c0 = small_turn(c_raw0)
         t_aw = small_turn(aw_raw)
@@ -408,6 +405,8 @@ def tile_rotelearningmemory_pa_kernel(
                 t_xb = x_turn(3)
             if i == 3:
                 t_q1 = small_turn(q_raw1)
+            if i == 1:
+                b_r = mm1(1)
             if i < 2:
                 t_w2 = w_turn(i + 2)
             if i < 3:
@@ -431,7 +430,6 @@ def tile_rotelearningmemory_pa_kernel(
                 g_c1 = small_lay(t_c1, "sv")
                 quant(g_c1[:], cc[:, HALF:T], cs[:, HALF:T])
             if i == 1:
-                b_r = mm1(1)
                 g_r = r_tile()
                 for n in range(4):
                     r_lay(g_r, b_r, n)
@@ -445,30 +443,34 @@ def tile_rotelearningmemory_pa_kernel(
                 g_q1 = small_lay(t_q1, "ss")
                 q_quant(1, g_q1)
 
-        lbp = []
-        for g in range(2):
-            lb_t = psum.tile([P, HALF], F32, name="lb_t", tag="bank")
-            nc.tensor.matmul(out=lb_t[:], lhsT=ones[:], rhs=lbz[:, g * 512 : (g + 1) * 512], start=True, stop=True)
-            lbp.append(lb_t)
-
-        plan = [(0, "s", "v"), (1, "v", "g"), (2, "s", "g"), (3, "s", "v"), None, (4, "v", "g"), (5, "s", "v"), None, (6, "s", "v"), (7, "s", "vv")]
-        to_scale = None
-        to_finish = None
-        for n in range(12):
+        plan = [(0, "s", "v"), (1, "s", "v"), (2, "s", "v"), (3, "s", "v"), None, (4, "s", "v"), (5, "s", "v"), None, (6, "s", "v"), (7, "s", "vv")]
+        first = None
+        second = None
+        for n in range(len(plan) + 2):
             if n < 8:
                 banks = gating256(2 + n // 4, n % 4)
-            if n < 10 and plan[n] is not None:
-                ybanks = y_tile(plan[n][0])
+            if first is not None and first[1] == "s":
+                nmean = nmean_s(first[4][1])
+            new = plan[n] if n < len(plan) else None
+            if new is not None:
+                ybanks = y_tile(new[0])
             if n < 8:
-                blend256(2 + n // 4, n % 4, banks, nc.gpsimd if n < 6 else nc.vector)
-            if to_finish is not None:
-                finish(*to_finish)
-                to_finish = None
-            if to_scale is not None:
-                k, fin, yb, nmean, rstd = to_scale
-                to_finish = (k, scale(yb, nmean), rstd, fin)
-                to_scale = None
-            if n < 10 and plan[n] is not None:
-                k, how, fin = plan[n]
-                nmean, rstd = stats_v(ybanks) if how == "v" else stats_s(ybanks)
-                to_scale = (k, fin, ybanks, nmean, rstd)
+                blend256(2 + n // 4, n % 4, banks, nc.gpsimd if n < 7 else nc.vector)
+            if first is not None and first[1] == "s":
+                s2 = squares_s(first[4][0], nmean)
+                rstd = rstd_of(s2[:], 1.0 / D)
+            if second is not None:
+                finish(*second)
+                second = None
+            if first is not None:
+                k, how, fin, yb, st = first
+                if how == "s":
+                    w_t = scale(yb, nmean[:], ALU.add)
+                else:
+                    rstd = rstd_of(st[:, 1:2], 1.0)
+                    w_t = scale(yb, st[:, 0:1], ALU.subtract)
+                second = (k, w_t, rstd, fin)
+                first = None
+            if new is not None:
+                k, how, fin = new
+                first = (k, how, fin, ybanks, stats_v(ybanks) if how == "v" else sums_s(ybanks))

@@ -29,13 +29,16 @@ def tile_rotelearningmemory_pa_kernel(
     def pairs(a):
         return a.rearrange("(i q e) k -> q i (e k)", q=P, e=2)
 
-    x_d = pairs(x.flatten_outer_dims())
-    q_d = pairs(query.flatten_outer_dims())
-    c_d = pairs(ctx.flatten_outer_dims())
+    def quads(a):
+        return a.rearrange("(h q e) k -> q h (e k)", q=P, e=4)
+
+    x_d = quads(x.flatten_outer_dims())
+    q_d = quads(query.flatten_outer_dims())
+    c_d = quads(ctx.flatten_outer_dims())
     aw_d = pairs(attn_out_w)
     ow_d = pairs(op_w)
     gw_d = pairs(gate_w)
-    out_d = out.flatten_outer_dims().rearrange("(i q e) d -> q i e d", q=P, e=2)
+    out_d = out.flatten_outer_dims().rearrange("(h q e) d -> q h e d", q=P, e=4)
 
     with ExitStack() as stack:
         stack.enter_context(tc.manual_schedule())
@@ -64,7 +67,7 @@ def tile_rotelearningmemory_pa_kernel(
         m1 = keep.tile([P, 8, HALF], F32)
         m_half = [m0, m1]
         vec = keep.tile([P, 256], BF16)
-        x_raw = keep.tile([P, 4, 2 * D], BF16)
+        x_raw = keep.tile([P, 2, 4 * D], BF16)
         lg_bc = keep.tile([P, D], BF16)
         lb_bc = keep.tile([P, D], BF16)
 
@@ -80,12 +83,14 @@ def tile_rotelearningmemory_pa_kernel(
         warm_out = keep.tile([P, 1], F32)
         nc.scalar.activation(out=warm_out[:], in_=warm_in[:], func=ACT.Sigmoid)
 
-        def load_act(src, th, nm, parts):
-            t = wraw.tile([P, 2, 2 * M], BF16, name=nm, tag="act")
-            n = 2 // parts
-            for j in range(parts):
-                nc.sync.dma_start(out=t[:, j * n : (j + 1) * n, :], in_=src[:, 2 * th + j * n : 2 * th + (j + 1) * n, :])
+        def load_act(src, th, nm):
+            t = wraw.tile([P, 4 * M], BF16, name=nm, tag="act")
+            nc.sync.dma_start(out=t[:], in_=src[:, th, :])
             return t
+
+        def load_x(th, j, parts):
+            w = 4 * D // parts
+            nc.sync.dma_start(out=x_raw[:, th, j * w : (j + 1) * w], in_=x_d[:, th, j * w : (j + 1) * w])
 
         def load_w(i):
             g_t = wraw.tile([P, 2 * (D + M)], BF16, name="gw_raw%d" % i, tag="gwraw")
@@ -94,20 +99,25 @@ def tile_rotelearningmemory_pa_kernel(
             nc.sync.dma_start(out=o_t[:], in_=ow_d[:, i, :])
             return g_t, o_t
 
-        c_raw0 = load_act(c_d, 0, "c_raw0", 2)
-        aw_raw = load_act(aw_d, 0, "aw_raw", 2)
-        nc.sync.dma_start(out=x_raw[:, 0, :], in_=x_d[:, 0, :])
+        c_raw0 = wraw.tile([P, 4 * M], BF16, name="c_raw0", tag="act")
+        for j in range(2):
+            nc.sync.dma_start(out=c_raw0[:, j * 2 * M : (j + 1) * 2 * M], in_=c_d[:, 0, j * 2 * M : (j + 1) * 2 * M])
+        aw_raw = wraw.tile([P, 2, 2 * M], BF16, name="aw_raw", tag="act")
+        nc.sync.dma_start(out=aw_raw[:], in_=aw_d[:])
         nc.sync.dma_start(out=vec[8:10, :], in_=attn_out_b.rearrange("(r c) -> r c", c=256))
         nc.sync.dma_start(out=vec[0:4, :], in_=gate_b.rearrange("(r c) -> r c", c=256))
         nc.sync.dma_start(out=vec[4:8, :], in_=op_b.rearrange("(r c) -> r c", c=256))
-        w_raw = [load_w(0)]
-        nc.sync.dma_start(out=x_raw[:, 1, :], in_=x_d[:, 1, :])
-        q_raw0 = load_act(q_d, 0, "q_raw0", 1)
-        w_raw.append(load_w(1))
-        c_raw1 = load_act(c_d, 1, "c_raw1", 1)
-        w_raw += [load_w(i) for i in range(2, 4)]
-        nc.sync.dma_start(out=x_raw[:, 2:4, :], in_=x_d[:, 2:4, :])
-        q_raw1 = load_act(q_d, 1, "q_raw1", 1)
+        w_raw = []
+        load_x(0, 0, 2)
+        w_raw.append(load_w(len(w_raw)))
+        load_x(0, 1, 2)
+        q_raw0 = load_act(q_d, 0, "q_raw0")
+        w_raw.append(load_w(len(w_raw)))
+        c_raw1 = load_act(c_d, 1, "c_raw1")
+        w_raw.append(load_w(len(w_raw)))
+        w_raw.append(load_w(len(w_raw)))
+        load_x(1, 0, 1)
+        q_raw1 = load_act(q_d, 1, "q_raw1")
         nc.sync.dma_start(out=lg_bc[:], in_=ln_g.partition_broadcast(P))
         nc.sync.dma_start(out=lb_bc[:], in_=ln_b.partition_broadcast(P))
 
@@ -136,8 +146,9 @@ def tile_rotelearningmemory_pa_kernel(
                 start=start, stop=stop,
             )
 
-        def words(t3):
-            return t3[:].rearrange("p i k -> p (i k)").bitcast(F32)
+        def words(t):
+            ap = t[:]
+            return (ap.rearrange("p i k -> p (i k)") if len(ap.shape) == 3 else ap).bitcast(F32)
 
         def small_turn(raw):
             w = words(raw)
@@ -240,9 +251,15 @@ def tile_rotelearningmemory_pa_kernel(
             return e_t
 
         def mul512(th, i, e, h_t, e_t):
-            for j in range(2):
-                c = slice(j * 256, (j + 1) * 256)
-                nc.gpsimd.tensor_tensor(out=m_half[th][:, 2 * i + e, c], in0=h_t[:, c], in1=e_t[:, c], op=ALU.mult)
+            out = m_half[th][:, 2 * i + e, :]
+            if th == 0 and i < 3:
+                for j in range(2):
+                    c = slice(j * 256, (j + 1) * 256)
+                    nc.gpsimd.tensor_tensor(out=out[:, c], in0=h_t[:, c], in1=e_t[:, c], op=ALU.mult)
+            elif th == 1:
+                nc.gpsimd.tensor_tensor(out=out, in0=h_t[:], in1=e_t[:], op=ALU.mult)
+            else:
+                nc.vector.tensor_tensor(out=out, in0=h_t[:], in1=e_t[:], op=ALU.mult)
 
         def gating256(quarter, i):
             th, ql = quarter // 2, quarter % 2
@@ -280,9 +297,9 @@ def tile_rotelearningmemory_pa_kernel(
             for g in range(2):
                 yp = psum.tile([P, 2, 256], F32, name="yp", tag="bank")
                 banks.append(yp)
-                o = (k % 2) * D + g * 512
+                o = (k % 4) * D + g * 512
                 nc.tensor.matmul(
-                    out=yp[:], lhsT=ident_b[:], rhs=x_raw[:, k // 2, o : o + 512].rearrange("p (a e) -> p e a", e=2),
+                    out=yp[:], lhsT=ident_b[:], rhs=x_raw[:, k // 4, o : o + 512].rearrange("p (a e) -> p e a", e=2),
                     start=True, stop=False,
                 )
                 for e in range(2):
@@ -343,11 +360,6 @@ def tile_rotelearningmemory_pa_kernel(
             return w_t
 
         def finish(k, w_t, rstd, how):
-            if how == "g":
-                nc.scalar.activation(out=w_t[:], in_=w_t[:], func=ACT.Copy, scale=rstd[:])
-                nc.gpsimd.tensor_tensor(out=w_t[:], in0=w_t[:], in1=lb_bc[:], op=ALU.add)
-                nc.sync.dma_start(out=out_d[:, k // 2, k % 2, :], in_=w_t[:])
-                return
             pieces = 2 if how == "vv" else 1
             width = D // pieces
             for c in range(pieces):
@@ -355,7 +367,7 @@ def tile_rotelearningmemory_pa_kernel(
                 nc.vector.scalar_tensor_tensor(
                     out=w_t[:, cols], in0=w_t[:, cols], scalar=rstd[:], in1=lb_bc[:, cols], op0=ALU.mult, op1=ALU.add
                 )
-                nc.sync.dma_start(out=out_d[:, k // 2, k % 2, cols], in_=w_t[:, cols])
+                nc.sync.dma_start(out=out_d[:, k // 4, k % 4, cols], in_=w_t[:, cols])
 
         t_c0 = small_turn(c_raw0)
         t_aw = small_turn(aw_raw)
@@ -397,14 +409,17 @@ def tile_rotelearningmemory_pa_kernel(
         t_w = w_turn(1)
 
         for i in range(4):
+            if i == 3:
+                t_q1 = small_turn(q_raw1)
+                g_q1 = small_lay(t_q1, "ss")
+                x_quant(1, 1)
+                q_quant(1, g_q1)
             banks = gating512(0, i)
             if i == 0:
                 t_c1 = small_turn(c_raw1)
             if i == 2:
                 t_xa = x_turn(2)
                 t_xb = x_turn(3)
-            if i == 3:
-                t_q1 = small_turn(q_raw1)
             if i == 1:
                 b_r = mm1(1)
             if i < 2:
@@ -438,24 +453,21 @@ def tile_rotelearningmemory_pa_kernel(
                 x_lay(2, t_xa, "ss")
                 x_lay(3, t_xb, "ss")
                 x_quant(1, 0)
-            if i == 3:
-                x_quant(1, 1)
-                g_q1 = small_lay(t_q1, "ss")
-                q_quant(1, g_q1)
 
-        plan = [(0, "s", "v"), (1, "s", "v"), (2, "s", "v"), (3, "s", "v"), None, (4, "s", "v"), (5, "s", "v"), None, (6, "s", "v"), (7, "s", "vv")]
+        steps = [((0,), (0, "s", "v")), ((1,), (1, "s", "v")), ((2,), (2, "s", "v")), ((3,), (3, "s", "v")), ((), (4, "s", "v")), ((), (5, "s", "v")), ((), (6, "s", "v")), ((), (7, "s", "vv"))]
         first = None
         second = None
-        for n in range(len(plan) + 2):
-            if n < 8:
-                banks = gating256(2 + n // 4, n % 4)
+        for groups, new in steps + [((), None), ((), None)]:
             if first is not None and first[1] == "s":
                 nmean = nmean_s(first[4][1])
-            new = plan[n] if n < len(plan) else None
+            for i in groups:
+                banks = gating512(1, i)
+                for e in range(2):
+                    e_t = diff512(1, i, e, banks)
+                    h_t = sig512(i, e, banks)
+                    mul512(1, i, e, h_t, e_t)
             if new is not None:
                 ybanks = y_tile(new[0])
-            if n < 8:
-                blend256(2 + n // 4, n % 4, banks, nc.gpsimd if n < 7 else nc.vector)
             if first is not None and first[1] == "s":
                 s2 = squares_s(first[4][0], nmean)
                 rstd = rstd_of(s2[:], 1.0 / D)

@@ -47,7 +47,7 @@ def tile_rotelearningmemory_pa_kernel(
         small = stack.enter_context(tc.tile_pool(name="small", bufs=8))
         wraw = stack.enter_context(tc.tile_pool(name="wraw", bufs=3))
         grp = stack.enter_context(tc.tile_pool(name="grp", bufs=3))
-        aux = stack.enter_context(tc.tile_pool(name="aux", bufs=2))
+        lny = stack.enter_context(tc.tile_pool(name="lny", bufs=2))
         lnw = stack.enter_context(tc.tile_pool(name="lnw", bufs=4))
         psum = stack.enter_context(tc.psum_pool(name="psum", bufs=8))
 
@@ -83,41 +83,41 @@ def tile_rotelearningmemory_pa_kernel(
         warm_out = keep.tile([P, 1], F32)
         nc.scalar.activation(out=warm_out[:], in_=warm_in[:], func=ACT.Sigmoid)
 
-        def load_act(src, th, nm):
-            t = wraw.tile([P, 4 * M], BF16, name=nm, tag="act")
-            nc.sync.dma_start(out=t[:], in_=src[:, th, :])
-            return t
-
-        def load_x(th, j, parts):
-            w = 4 * D // parts
-            nc.sync.dma_start(out=x_raw[:, th, j * w : (j + 1) * w], in_=x_d[:, th, j * w : (j + 1) * w])
-
         def load_w(i):
             g_t = wraw.tile([P, 2 * (D + M)], BF16, name="gw_raw%d" % i, tag="gwraw")
             nc.sync.dma_start(out=g_t[:], in_=gw_d[:, i, :])
             o_t = wraw.tile([P, 2 * M], BF16, name="ow_raw%d" % i, tag="owraw")
             nc.sync.dma_start(out=o_t[:], in_=ow_d[:, i, :])
-            return g_t, o_t
+            return g_t[:].bitcast(F32), o_t[:].bitcast(F32)
 
-        c_raw0 = wraw.tile([P, 4 * M], BF16, name="c_raw0", tag="act")
-        for j in range(2):
-            nc.sync.dma_start(out=c_raw0[:, j * 2 * M : (j + 1) * 2 * M], in_=c_d[:, 0, j * 2 * M : (j + 1) * 2 * M])
-        aw_raw = wraw.tile([P, 2, 2 * M], BF16, name="aw_raw", tag="act")
-        nc.sync.dma_start(out=aw_raw[:], in_=aw_d[:])
+        def load_x(th, j, parts):
+            w = 4 * D // parts
+            nc.sync.dma_start(out=x_raw[:, th, j * w : (j + 1) * w], in_=x_d[:, th, j * w : (j + 1) * w])
+
+        def load_512(src, th, nm, parts):
+            t = wraw.tile([P, 4 * M], BF16, name=nm, tag="act")
+            w = 4 * M // parts
+            for j in range(parts):
+                nc.sync.dma_start(out=t[:, j * w : (j + 1) * w], in_=src[:, th, j * w : (j + 1) * w])
+            return t[:].bitcast(F32)
+
+        c_raw0 = load_512(c_d, 0, "c_raw0", 2)
+        aw_t = wraw.tile([P, 4 * M], BF16, name="aw_t", tag="act")
+        nc.sync.dma_start(out=aw_t[:].rearrange("p (i k) -> p i k", i=2), in_=aw_d[:])
+        aw_raw = aw_t[:].bitcast(F32)
         nc.sync.dma_start(out=vec[8:10, :], in_=attn_out_b.rearrange("(r c) -> r c", c=256))
         nc.sync.dma_start(out=vec[0:4, :], in_=gate_b.rearrange("(r c) -> r c", c=256))
         nc.sync.dma_start(out=vec[4:8, :], in_=op_b.rearrange("(r c) -> r c", c=256))
-        w_raw = []
         load_x(0, 0, 2)
-        w_raw.append(load_w(len(w_raw)))
+        w_raw = [load_w(0)]
         load_x(0, 1, 2)
-        q_raw0 = load_act(q_d, 0, "q_raw0")
-        w_raw.append(load_w(len(w_raw)))
-        c_raw1 = load_act(c_d, 1, "c_raw1")
-        w_raw.append(load_w(len(w_raw)))
-        w_raw.append(load_w(len(w_raw)))
+        q_raw0 = load_512(q_d, 0, "q_raw0", 1)
+        w_raw.append(load_w(1))
+        c_raw1 = load_512(c_d, 1, "c_raw1", 1)
+        w_raw.append(load_w(2))
+        w_raw.append(load_w(3))
         load_x(1, 0, 1)
-        q_raw1 = load_act(q_d, 1, "q_raw1")
+        q_raw1 = load_512(q_d, 1, "q_raw1", 1)
         nc.sync.dma_start(out=lg_bc[:], in_=ln_g.partition_broadcast(P))
         nc.sync.dma_start(out=lb_bc[:], in_=ln_b.partition_broadcast(P))
 
@@ -146,28 +146,24 @@ def tile_rotelearningmemory_pa_kernel(
                 start=start, stop=stop,
             )
 
-        def words(t):
-            ap = t[:]
-            return (ap.rearrange("p i k -> p (i k)") if len(ap.shape) == 3 else ap).bitcast(F32)
+        def turn_512(words):
+            return [turn(words, il * M, M // 2) for il in range(2)]
 
-        def small_turn(raw):
-            w = words(raw)
-            return [turn(w, il * M, M // 2) for il in range(2)]
-
-        def small_lay(tps, engs):
-            g = grp.tile([P, 4 * HALF], BF16, name="g_small", tag="ga", align_bytes=64)
+        def lay_512(tps, eng):
+            g = grp.tile([P, 4 * HALF], BF16, name="g_512", tag="ga", align_bytes=64)
             for il in range(2):
-                lay(tps[il], g[:, il * 1024 : (il + 1) * 1024], engs[il])
+                lay(tps[il], g[:, il * 1024 : (il + 1) * 1024], eng)
             return g
 
-        def x_turn(i):
-            w = words(x_raw)
-            return [turn(w, i * D + g * 256, D // 2) for g in range(2)]
+        x_words = x_raw[:].rearrange("p h k -> p (h k)").bitcast(F32)
 
-        def x_lay(i, tps, engs):
+        def x_turn(i):
+            return [turn(x_words, i * D + g * 256, D // 2) for g in range(2)]
+
+        def x_lay(i, tps):
             for g in range(2):
                 a = ((i // 2 * 2 + g) * HALF + i % 2 * 256) * 4
-                lay(tps[g], gx[:, a : a + 1024], engs[g])
+                lay(tps[g], gx[:, a : a + 1024], "s")
 
         def x_quant(th, g):
             a = th * 1536 + g * 512
@@ -178,17 +174,16 @@ def tile_rotelearningmemory_pa_kernel(
             quant(g[:], gc[:, a : a + 512], gs[:, a : a + 512])
 
         def w_turn(i):
-            g_t, o_t = w_raw[i]
-            tps = [turn(g_t[:].bitcast(F32), s * 256, (D + M) // 2) for s in range(3)]
-            tps.append(turn(o_t[:].bitcast(F32), 0, M // 2))
-            return tps
+            g_w, o_w = w_raw[i]
+            return [turn(g_w, s * 256, (D + M) // 2) for s in range(3)] + [turn(o_w, 0, M // 2)]
 
         def w_tile():
             g_w = grp.tile([P, 4 * 4 * 256], BF16, name="g_w", tag="gw", align_bytes=64)
             return g_w
 
-        def w_lay(g, tps, s, eng):
-            lay(tps[s], g[:, s * 1024 : (s + 1) * 1024], eng)
+        def w_lay(g, tps, h, engs):
+            for s in (2 * h, 2 * h + 1):
+                lay(tps[s], g[:, s * 1024 : (s + 1) * 1024], engs[s])
 
         def w_quant(i, g, h):
             a = i * 1024 + h * 512
@@ -204,23 +199,20 @@ def tile_rotelearningmemory_pa_kernel(
                 banks.append(p1)
             return banks
 
-        def r_tile():
+        def r_lay(banks):
             g_r = grp.tile([P, HALF, 4], BF16, name="g_r", tag="ga", align_bytes=64)
+            for n in range(4):
+                nc.vector.tensor_tensor(
+                    out=g_r[:, n * P : (n + 1) * P, :], in0=banks[n][:].rearrange("p t c -> p c t"),
+                    in1=ab[:].unsqueeze(1).to_broadcast([P, P, 4]), op=ALU.add,
+                )
             return g_r
 
-        def r_lay(g_r, banks, n):
-            nc.vector.tensor_tensor(
-                out=g_r[:, n * P : (n + 1) * P, :], in0=banks[n][:].rearrange("p t c -> p c t"),
-                in1=ab[:].unsqueeze(1).to_broadcast([P, P, 4]), op=ALU.add,
-            )
-
         def r_quant(th, g_r):
-            quant(
-                g_r[:].rearrange("p c t -> p (c t)"),
-                rc[:, th * HALF : (th + 1) * HALF], rs[:, th * HALF : (th + 1) * HALF],
-            )
+            tok = slice(th * HALF, (th + 1) * HALF)
+            quant(g_r[:].rearrange("p c t -> p (c t)"), rc[:, tok], rs[:, tok])
 
-        def gating512(th, i):
+        def gating(th, i):
             tok = slice(th * HALF, (th + 1) * HALF)
             banks = []
             for e in range(2):
@@ -235,13 +227,13 @@ def tile_rotelearningmemory_pa_kernel(
                 banks.append((p2, p3))
             return banks
 
-        def sig512(i, e, banks):
+        def sigm(i, e, banks):
             d = 2 * i + e
             h_t = gwork.tile([P, HALF], F32, name="h_t", tag="h")
             nc.scalar.activation(out=h_t[:], in_=banks[e][1][:], func=ACT.Sigmoid, bias=ngb[:, d : d + 1], scale=-1.0)
             return h_t
 
-        def diff512(th, i, e, banks):
+        def diff(th, i, e, banks):
             d = 2 * i + e
             e_t = gwork.tile([P, HALF], F32, name="e_t", tag="e")
             nc.vector.scalar_tensor_tensor(
@@ -250,46 +242,10 @@ def tile_rotelearningmemory_pa_kernel(
             )
             return e_t
 
-        def mul512(th, i, e, h_t, e_t):
-            out = m_half[th][:, 2 * i + e, :]
-            if th == 0 and i < 3:
-                for j in range(2):
-                    c = slice(j * 256, (j + 1) * 256)
-                    nc.gpsimd.tensor_tensor(out=out[:, c], in0=h_t[:, c], in1=e_t[:, c], op=ALU.mult)
-            elif th == 1:
-                nc.gpsimd.tensor_tensor(out=out, in0=h_t[:], in1=e_t[:], op=ALU.mult)
-            else:
-                nc.vector.tensor_tensor(out=out, in0=h_t[:], in1=e_t[:], op=ALU.mult)
-
-        def gating256(quarter, i):
-            th, ql = quarter // 2, quarter % 2
-            tok = slice(quarter * 256, (quarter + 1) * 256)
-            p2 = psum.tile([P, 2, 256], F32, name="p2q", tag="bank")
-            p3 = psum.tile([P, 2, 256], F32, name="p3q", tag="bank")
-            for e in range(2):
-                a = (i * 4 + 3) * 256 + e * P
-                mx(p2[:, e, :], wc[:, a : a + P], ws[:, a : a + P], rc[:, tok], rs[:, tok], True, True)
-            for e in range(2):
-                for s in range(3):
-                    a = (i * 4 + s) * 256 + e * P
-                    b = (th * 3 + s) * HALF + ql * 256
-                    mx(p3[:, e, :], wc[:, a : a + P], ws[:, a : a + P], gc[:, b : b + 256], gs[:, b : b + 256], s == 0, s == 2)
-            return p2, p3
-
-        def blend256(quarter, i, banks, eng):
-            th, ql = quarter // 2, quarter % 2
-            p2, p3 = banks
-            cols = slice(ql * 256, (ql + 1) * 256)
-            h_t = gwork.tile([P, 2, 256], F32, name="h_t", tag="h")
-            e_t = gwork.tile([P, 2, 256], F32, name="e_t", tag="e")
-            for e in range(2):
-                d = 2 * i + e
-                nc.scalar.activation(out=h_t[:, e, :], in_=p3[:, e, :], func=ACT.Sigmoid, bias=ngb[:, d : d + 1], scale=-1.0)
-                nc.vector.scalar_tensor_tensor(
-                    out=e_t[:, e, :], in0=p2[:, e, :], scalar=ob[:, d : d + 1],
-                    in1=gx5[:, th, i // 2, cols, 2 * (i % 2) + e], op0=ALU.add, op1=ALU.subtract,
-                )
-            eng.tensor_tensor(out=m_half[th][:, 2 * i : 2 * i + 2, cols], in0=h_t[:], in1=e_t[:], op=ALU.mult)
+        def mul(th, i, e, h_t, e_t):
+            late = i >= 2 if th == 0 else (i, e) == (3, 1)
+            eng = nc.vector if late else nc.gpsimd
+            eng.tensor_tensor(out=m_half[th][:, 2 * i + e, :], in0=h_t[:], in1=e_t[:], op=ALU.mult)
 
         def y_tile(k):
             th, j = k // 4, k % 4
@@ -297,9 +253,9 @@ def tile_rotelearningmemory_pa_kernel(
             for g in range(2):
                 yp = psum.tile([P, 2, 256], F32, name="yp", tag="bank")
                 banks.append(yp)
-                o = (k % 4) * D + g * 512
+                o = j * D + g * 512
                 nc.tensor.matmul(
-                    out=yp[:], lhsT=ident_b[:], rhs=x_raw[:, k // 4, o : o + 512].rearrange("p (a e) -> p e a", e=2),
+                    out=yp[:], lhsT=ident_b[:], rhs=x_raw[:, th, o : o + 512].rearrange("p (a e) -> p e a", e=2),
                     start=True, stop=False,
                 )
                 for e in range(2):
@@ -310,23 +266,8 @@ def tile_rotelearningmemory_pa_kernel(
                         )
             return banks
 
-        def rstd_of(var, scl):
-            ve = small.tile([P, 1], F32, name="ve", tag="ve")
-            nc.gpsimd.tensor_scalar(out=ve[:], in0=var, scalar1=scl, scalar2=LN_EPS, op0=ALU.mult, op1=ALU.add)
-            rstd = small.tile([P, 1], F32, name="rstd", tag="rstd")
-            nc.gpsimd.tensor_tensor(out=rstd[:], in0=ve[:], in1=mhalf[:], op=ALU.pow)
-            return rstd
-
-        def stats_v(banks):
-            stats = small.tile([P, 2, 6], F32, name="stats", tag="stats")
-            for g in range(2):
-                nc.vector.bn_stats(out=stats[:, g, :], in_=banks[g][:].rearrange("p e a -> p (e a)"))
-            mv = small.tile([P, 2], F32, name="mv", tag="mv")
-            nc.vector.bn_aggr(out=mv[:], in_=stats[:].rearrange("p g s -> p (g s)"))
-            return mv
-
-        def sums_s(banks):
-            y_t = aux.tile([P, D], F32, name="y_t", tag="y")
+        def sums(banks):
+            y_t = lny.tile([P, D], F32, name="y_t", tag="y")
             s1 = small.tile([P, 2], F32, name="s1", tag="s1")
             for g in range(2):
                 nc.scalar.activation(
@@ -335,32 +276,39 @@ def tile_rotelearningmemory_pa_kernel(
                 )
             return y_t, s1
 
-        def nmean_s(s1):
+        def minus_mean(s1):
             nmean = small.tile([P, 1], F32, name="nmean", tag="nmean")
             nc.scalar.activation(out=nmean[:], in_=s1[:, 0:1], func=ACT.Identity, bias=s1[:, 1:2], scale=1.0)
             return nmean
 
-        def squares_s(y_t, nmean):
-            junk = aux.tile([P, D], BF16, name="junk", tag="junk", bufs=1)
+        def squares(y_t, nmean):
+            junk = lny.tile([P, D], BF16, name="junk", tag="junk")
             s2 = small.tile([P, 1], F32, name="s2", tag="s2")
             nc.scalar.activation(
                 out=junk[:], in_=y_t[:], func=ACT.Square, bias=nmean[:], scale=-1.0 * D, accum_out=s2[:]
             )
             return s2
 
-        def scale(banks, shift, op):
+        def rstd_of(s2):
+            ve = small.tile([P, 1], F32, name="ve", tag="ve")
+            nc.gpsimd.tensor_scalar(out=ve[:], in0=s2[:], scalar1=1.0 / D, scalar2=LN_EPS, op0=ALU.mult, op1=ALU.add)
+            rstd = small.tile([P, 1], F32, name="rstd", tag="rstd")
+            nc.gpsimd.tensor_tensor(out=rstd[:], in0=ve[:], in1=mhalf[:], op=ALU.pow)
+            return rstd
+
+        def scale(banks, nmean):
             w_t = lnw.tile([P, D], F32, name="w_t", tag="w")
             for g in range(2):
                 nc.vector.scalar_tensor_tensor(
                     out=w_t[:, g * 512 : (g + 1) * 512].rearrange("p (a e) -> p a e", e=2),
-                    in0=banks[g][:].rearrange("p e a -> p a e"), scalar=shift,
+                    in0=banks[g][:].rearrange("p e a -> p a e"), scalar=nmean[:],
                     in1=lg_bc[:, g * 512 : (g + 1) * 512].rearrange("p (a e) -> p a e", e=2),
-                    op0=op, op1=ALU.mult,
+                    op0=ALU.add, op1=ALU.mult,
                 )
             return w_t
 
-        def finish(k, w_t, rstd, how):
-            pieces = 2 if how == "vv" else 1
+        def finish(k, w_t, rstd):
+            pieces = 2 if k == 7 else 1
             width = D // pieces
             for c in range(pieces):
                 cols = slice(c * width, (c + 1) * width)
@@ -369,10 +317,10 @@ def tile_rotelearningmemory_pa_kernel(
                 )
                 nc.sync.dma_start(out=out_d[:, k // 4, k % 4, cols], in_=w_t[:, cols])
 
-        t_c0 = small_turn(c_raw0)
-        t_aw = small_turn(aw_raw)
-        g_c0 = small_lay(t_c0, "sv")
-        g_aw = small_lay(t_aw, "sv")
+        t_c0 = turn_512(c_raw0)
+        t_aw = turn_512(aw_raw)
+        g_c0 = lay_512(t_c0, "s")
+        g_aw = lay_512(t_aw, "s")
         quant(g_c0[:], cc[:, 0:HALF], cs[:, 0:HALF])
         quant(g_aw[:], wa[:], was[:])
         t_xa = x_turn(0)
@@ -386,103 +334,85 @@ def tile_rotelearningmemory_pa_kernel(
         ob = keep.tile([P, 8], F32)
         nc.vector.tensor_copy(out=ob[:], in_=vt_b[:, 8:16])
         b_r = mm1(0)
-        x_lay(0, t_xa, "ss")
-        g_r = r_tile()
-        r_lay(g_r, b_r, 0)
-        r_lay(g_r, b_r, 1)
+        x_lay(0, t_xa)
+        g_r = r_lay(b_r)
         t_w = w_turn(0)
-        r_lay(g_r, b_r, 2)
-        r_lay(g_r, b_r, 3)
         g_w = w_tile()
-        for s in range(4):
-            w_lay(g_w, t_w, s, "s")
+        w_lay(g_w, t_w, 0, "ssvs")
+        w_lay(g_w, t_w, 1, "ssvs")
         t_xb = x_turn(1)
-        t_q0 = small_turn(q_raw0)
+        x_lay(1, t_xb)
+        t_q = turn_512(q_raw0)
+        g_q = lay_512(t_q, "s")
         r_quant(0, g_r)
-        x_lay(1, t_xb, "ss")
         w_quant(0, g_w, 0)
         w_quant(0, g_w, 1)
         x_quant(0, 0)
         x_quant(0, 1)
-        g_q0 = small_lay(t_q0, "ss")
-        q_quant(0, g_q0)
+        q_quant(0, g_q)
         t_w = w_turn(1)
 
         for i in range(4):
             if i == 3:
-                t_q1 = small_turn(q_raw1)
-                g_q1 = small_lay(t_q1, "ss")
+                t_q = turn_512(q_raw1)
+                g_q = lay_512(t_q, "s")
                 x_quant(1, 1)
-                q_quant(1, g_q1)
-            banks = gating512(0, i)
+                q_quant(1, g_q)
+            banks = gating(0, i)
             if i == 0:
-                t_c1 = small_turn(c_raw1)
+                t_c1 = turn_512(c_raw1)
+            if i == 1:
+                b_r = mm1(1)
             if i == 2:
                 t_xa = x_turn(2)
                 t_xb = x_turn(3)
-            if i == 1:
-                b_r = mm1(1)
             if i < 2:
-                t_w2 = w_turn(i + 2)
+                t_next = w_turn(i + 2)
             if i < 3:
                 g_w = w_tile()
-                for s in range(3):
-                    w_lay(g_w, t_w, s, "s")
-                w_lay(g_w, t_w, 3, "s")
-            e0 = diff512(0, i, 0, banks)
-            h0 = sig512(i, 0, banks)
-            mul512(0, i, 0, h0, e0)
-            if i < 3:
-                w_quant(i + 1, g_w, 0)
-            e1 = diff512(0, i, 1, banks)
-            h1 = sig512(i, 1, banks)
-            mul512(0, i, 1, h1, e1)
-            if i < 3:
-                w_quant(i + 1, g_w, 1)
+            e_ts = []
+            for e in range(2):
+                if i < 3:
+                    w_lay(g_w, t_w, e, "ssss")
+                    w_quant(i + 1, g_w, e)
+                e_ts.append(diff(0, i, e, banks))
+            for e in range(2):
+                mul(0, i, e, sigm(i, e, banks), e_ts[e])
             if i < 2:
-                t_w = t_w2
+                t_w = t_next
             if i == 0:
-                g_c1 = small_lay(t_c1, "sv")
+                g_c1 = lay_512(t_c1, "v")
                 quant(g_c1[:], cc[:, HALF:T], cs[:, HALF:T])
             if i == 1:
-                g_r = r_tile()
-                for n in range(4):
-                    r_lay(g_r, b_r, n)
+                g_r = r_lay(b_r)
             if i == 2:
                 r_quant(1, g_r)
-                x_lay(2, t_xa, "ss")
-                x_lay(3, t_xb, "ss")
+                x_lay(2, t_xa)
+                x_lay(3, t_xb)
                 x_quant(1, 0)
 
-        steps = [((0,), (0, "s", "v")), ((1,), (1, "s", "v")), ((2,), (2, "s", "v")), ((3,), (3, "s", "v")), ((), (4, "s", "v")), ((), (5, "s", "v")), ((), (6, "s", "v")), ((), (7, "s", "vv"))]
         first = None
         second = None
-        for groups, new in steps + [((), None), ((), None)]:
-            if first is not None and first[1] == "s":
-                nmean = nmean_s(first[4][1])
-            for i in groups:
-                banks = gating512(1, i)
-                for e in range(2):
-                    e_t = diff512(1, i, e, banks)
-                    h_t = sig512(i, e, banks)
-                    mul512(1, i, e, h_t, e_t)
-            if new is not None:
-                ybanks = y_tile(new[0])
-            if first is not None and first[1] == "s":
-                s2 = squares_s(first[4][0], nmean)
-                rstd = rstd_of(s2[:], 1.0 / D)
+        for n in range(10):
+            if n < 4:
+                banks = gating(1, n)
+            if n < 8:
+                ybanks = y_tile(n)
+            if n < 4:
+                h_ts = [sigm(n, e, banks) for e in range(2)]
+            if n < 8:
+                y_t, s1 = sums(ybanks)
+            if first is not None:
+                s2 = squares(first[2], first[3])
+            if n < 8:
+                nmean = minus_mean(s1)
+            if n < 4:
+                mul(1, n, 0, h_ts[0], diff(1, n, 0, banks))
+            if first is not None:
+                scaled = (first[0], scale(first[1], first[3]))
+            if n < 4:
+                mul(1, n, 1, h_ts[1], diff(1, n, 1, banks))
             if second is not None:
                 finish(*second)
-                second = None
-            if first is not None:
-                k, how, fin, yb, st = first
-                if how == "s":
-                    w_t = scale(yb, nmean[:], ALU.add)
-                else:
-                    rstd = rstd_of(st[:, 1:2], 1.0)
-                    w_t = scale(yb, st[:, 0:1], ALU.subtract)
-                second = (k, w_t, rstd, fin)
-                first = None
-            if new is not None:
-                k, how, fin = new
-                first = (k, how, fin, ybanks, stats_v(ybanks) if how == "v" else sums_s(ybanks))
+            second = scaled + (rstd_of(s2),) if first is not None else None
+            first = (n, ybanks, y_t, nmean) if n < 8 else None

@@ -267,7 +267,7 @@ def tile_rotelearningmemory_pa_kernel(
             return banks
 
         def sums(banks):
-            y_t = lny.tile([P, D], F32, name="y_t", tag="y")
+            y_t = lny.tile([P, D], F32, name="y_t", tag="y", bufs=3)
             s1 = small.tile([P, 2], F32, name="s1", tag="s1")
             for g in range(2):
                 nc.scalar.activation(

@@ -95,14 +95,14 @@ def tile_rotelearningmemory_pa_kernel(
             nc.sync.dma_start(out=x_raw[:, th, j * w : (j + 1) * w], in_=x_d[:, th, j * w : (j + 1) * w])
 
         def load_512(src, th, nm, parts):
-            t = wraw.tile([P, 4 * M], BF16, name=nm, tag="act")
+            t = wraw.tile([P, 4 * M], BF16, name=nm, tag="act", bufs=4)
             w = 4 * M // parts
             for j in range(parts):
                 nc.sync.dma_start(out=t[:, j * w : (j + 1) * w], in_=src[:, th, j * w : (j + 1) * w])
             return t[:].bitcast(F32)
 
         c_raw0 = load_512(c_d, 0, "c_raw0", 2)
-        aw_t = wraw.tile([P, 4 * M], BF16, name="aw_t", tag="act")
+        aw_t = wraw.tile([P, 4 * M], BF16, name="aw_t", tag="act", bufs=4)
         nc.sync.dma_start(out=aw_t[:].rearrange("p (i k) -> p i k", i=2), in_=aw_d[:])
         aw_raw = aw_t[:].bitcast(F32)
         nc.sync.dma_start(out=vec[8:10, :], in_=attn_out_b.rearrange("(r c) -> r c", c=256))
@@ -112,11 +112,11 @@ def tile_rotelearningmemory_pa_kernel(
         w_raw = [load_w(0)]
         load_x(0, 1, 2)
         q_raw0 = load_512(q_d, 0, "q_raw0", 1)
-        w_raw.append(load_w(1))
         c_raw1 = load_512(c_d, 1, "c_raw1", 1)
+        w_raw.append(load_w(1))
         w_raw.append(load_w(2))
-        w_raw.append(load_w(3))
         load_x(1, 0, 1)
+        w_raw.append(load_w(3))
         q_raw1 = load_512(q_d, 1, "q_raw1", 1)
         nc.sync.dma_start(out=lg_bc[:], in_=ln_g.partition_broadcast(P))
         nc.sync.dma_start(out=lb_bc[:], in_=ln_b.partition_broadcast(P))
@@ -160,10 +160,10 @@ def tile_rotelearningmemory_pa_kernel(
         def x_turn(i):
             return [turn(x_words, i * D + g * 256, D // 2) for g in range(2)]
 
-        def x_lay(i, tps):
+        def x_lay(i, tps, engs):
             for g in range(2):
                 a = ((i // 2 * 2 + g) * HALF + i % 2 * 256) * 4
-                lay(tps[g], gx[:, a : a + 1024], "s")
+                lay(tps[g], gx[:, a : a + 1024], engs[g])
 
         def x_quant(th, g):
             a = th * 1536 + g * 512
@@ -178,7 +178,7 @@ def tile_rotelearningmemory_pa_kernel(
             return [turn(g_w, s * 256, (D + M) // 2) for s in range(3)] + [turn(o_w, 0, M // 2)]
 
         def w_tile():
-            g_w = grp.tile([P, 4 * 4 * 256], BF16, name="g_w", tag="gw", align_bytes=64)
+            g_w = grp.tile([P, 4 * 4 * 256], BF16, name="g_w", tag="gw", align_bytes=64, bufs=2)
             return g_w
 
         def w_lay(g, tps, h, engs):
@@ -308,7 +308,7 @@ def tile_rotelearningmemory_pa_kernel(
             return w_t
 
         def finish(k, w_t, rstd):
-            pieces = 2 if k == 7 else 1
+            pieces = 2 if k >= 6 else 1
             width = D // pieces
             for c in range(pieces):
                 cols = slice(c * width, (c + 1) * width)
@@ -334,14 +334,14 @@ def tile_rotelearningmemory_pa_kernel(
         ob = keep.tile([P, 8], F32)
         nc.vector.tensor_copy(out=ob[:], in_=vt_b[:, 8:16])
         b_r = mm1(0)
-        x_lay(0, t_xa)
+        x_lay(0, t_xa, "ss")
         g_r = r_lay(b_r)
         t_w = w_turn(0)
         g_w = w_tile()
         w_lay(g_w, t_w, 0, "ssvs")
         w_lay(g_w, t_w, 1, "ssvs")
         t_xb = x_turn(1)
-        x_lay(1, t_xb)
+        x_lay(1, t_xb, "ss")
         t_q = turn_512(q_raw0)
         g_q = lay_512(t_q, "s")
         r_quant(0, g_r)
@@ -350,6 +350,9 @@ def tile_rotelearningmemory_pa_kernel(
         x_quant(0, 0)
         x_quant(0, 1)
         q_quant(0, g_q)
+        t_c1 = turn_512(c_raw1)
+        g_c1 = lay_512(t_c1, "s")
+        quant(g_c1[:], cc[:, HALF:T], cs[:, HALF:T])
         t_w = w_turn(1)
 
         for i in range(4):
@@ -360,35 +363,29 @@ def tile_rotelearningmemory_pa_kernel(
                 q_quant(1, g_q)
             banks = gating(0, i)
             if i == 0:
-                t_c1 = turn_512(c_raw1)
-            if i == 1:
                 b_r = mm1(1)
-            if i == 2:
-                t_xa = x_turn(2)
-                t_xb = x_turn(3)
+            if i == 1 or i == 2:
+                t_x = x_turn(i + 1)
             if i < 2:
                 t_next = w_turn(i + 2)
             if i < 3:
                 g_w = w_tile()
-            e_ts = []
-            for e in range(2):
-                if i < 3:
-                    w_lay(g_w, t_w, e, "ssss")
-                    w_quant(i + 1, g_w, e)
-                e_ts.append(diff(0, i, e, banks))
+            e_ts = [diff(0, i, 0, banks)]
+            for h in range(2 if i < 3 else 0):
+                w_lay(g_w, t_w, h, "ssss")
+                w_quant(i + 1, g_w, h)
+            e_ts.append(diff(0, i, 1, banks))
             for e in range(2):
                 mul(0, i, e, sigm(i, e, banks), e_ts[e])
             if i < 2:
                 t_w = t_next
             if i == 0:
-                g_c1 = lay_512(t_c1, "v")
-                quant(g_c1[:], cc[:, HALF:T], cs[:, HALF:T])
-            if i == 1:
                 g_r = r_lay(b_r)
-            if i == 2:
+            if i == 1:
                 r_quant(1, g_r)
-                x_lay(2, t_xa)
-                x_lay(3, t_xb)
+                x_lay(2, t_x, "sv")
+            if i == 2:
+                x_lay(3, t_x, "ss")
                 x_quant(1, 0)
 
         first = None

from contextlib import ExitStack

import concourse.mybir as mybir
from concourse.masks import make_identity

F32 = mybir.dt.float32
BF16 = mybir.dt.bfloat16
U32 = mybir.dt.uint32
U8 = mybir.dt.uint8
FP8X4 = mybir.dt.float8_e4m3fn_x4
ACT = mybir.ActivationFunctionType
ALU = mybir.AluOpType

P = 128
T = 1024
D = 1024
M = 512
HALF = 512
LN_EPS = 1e-5

FLOPS = 2 * T * (M * M + M * D + (D + M) * D)


def tile_rotelearningmemory_pa_kernel(
    tc, x, query, ctx, attn_out_w, attn_out_b, op_w, op_b, gate_w, gate_b, ln_g, ln_b, out
):
    nc = tc.nc

    def pairs(a):
        return a.rearrange("(i q e) k -> q i (e k)", q=P, e=2)

    def quads(a):
        return a.rearrange("(h q e) k -> q h (e k)", q=P, e=4)

    x_d = quads(x.flatten_outer_dims())
    q_d = quads(query.flatten_outer_dims())
    c_d = quads(ctx.flatten_outer_dims())
    aw_d = pairs(attn_out_w)
    ow_d = pairs(op_w)
    gw_d = pairs(gate_w)
    out_d = out.flatten_outer_dims().rearrange("(h q e) d -> q h e d", q=P, e=4)

    with ExitStack() as stack:
        stack.enter_context(tc.manual_schedule())
        keep = stack.enter_context(tc.tile_pool(name="keep", bufs=1))
        gwork = stack.enter_context(tc.tile_pool(name="gwork", bufs=4))
        small = stack.enter_context(tc.tile_pool(name="small", bufs=8))
        wraw = stack.enter_context(tc.tile_pool(name="wraw", bufs=3))
        grp = stack.enter_context(tc.tile_pool(name="grp", bufs=3))
        lny = stack.enter_context(tc.tile_pool(name="lny", bufs=2))
        lnw = stack.enter_context(tc.tile_pool(name="lnw", bufs=4))
        psum = stack.enter_context(tc.psum_pool(name="psum", bufs=8))

        cc = keep.tile([P, T], U32, align_bytes=64)
        cs = keep.tile([P, T], U8, align_bytes=64)
        wa = keep.tile([P, M], U32, align_bytes=64)
        was = keep.tile([P, M], U8, align_bytes=64)
        gc = keep.tile([P, 2 * 3 * HALF], U32, align_bytes=64)
        gs = keep.tile([P, 2 * 3 * HALF], U8, align_bytes=64)
        wc = keep.tile([P, 4 * 4 * 256], U32, align_bytes=64)
        ws = keep.tile([P, 4 * 4 * 256], U8, align_bytes=64)
        rc = keep.tile([P, T], U32, align_bytes=64)
        rs = keep.tile([P, T], U8, align_bytes=64)
        gx = keep.tile([P, 2 * 2 * HALF * 4], BF16, align_bytes=64)
        gx5 = gx[:].rearrange("p (h g c t) -> p h g c t", h=2, g=2, t=4)
        m0 = keep.tile([P, 8, HALF], F32)
        m1 = keep.tile([P, 8, HALF], F32)
        m_half = [m0, m1]
        vec = keep.tile([P, 256], BF16)
        x_raw = keep.tile([P, 2, 4 * D], BF16)
        lg_bc = keep.tile([P, D], BF16)
        lb_bc = keep.tile([P, D], BF16)

        nc.vector.memset(vec[:].bitcast(F32), 0.0)
        ident_f = keep.tile([P, P], F32)
        make_identity(nc, ident_f[:])
        ident_b = keep.tile([P, P], BF16)
        make_identity(nc, ident_b[:])
        mhalf = keep.tile([P, 1], F32)
        nc.gpsimd.memset(mhalf[:], -0.5)
        warm_in = keep.tile([P, 1], F32)
        nc.vector.memset(warm_in[:], 0.0)
        warm_out = keep.tile([P, 1], F32)
        nc.scalar.activation(out=warm_out[:], in_=warm_in[:], func=ACT.Sigmoid)

        def load_w(i):
            g_t = wraw.tile([P, 2 * (D + M)], BF16, name="gw_raw%d" % i, tag="gwraw")
            nc.sync.dma_start(out=g_t[:], in_=gw_d[:, i, :])
            o_t = wraw.tile([P, 2 * M], BF16, name="ow_raw%d" % i, tag="owraw")
            nc.sync.dma_start(out=o_t[:], in_=ow_d[:, i, :])
            return g_t[:].bitcast(F32), o_t[:].bitcast(F32)

        def load_x(th, j, parts):
            w = 4 * D // parts
            nc.sync.dma_start(out=x_raw[:, th, j * w : (j + 1) * w], in_=x_d[:, th, j * w : (j + 1) * w])

        def load_512(src, th, nm, parts):
            t = wraw.tile([P, 4 * M], BF16, name=nm, tag="act", bufs=4)
            w = 4 * M // parts
            for j in range(parts):
                nc.sync.dma_start(out=t[:, j * w : (j + 1) * w], in_=src[:, th, j * w : (j + 1) * w])
            return t[:].bitcast(F32)

        c_raw0 = load_512(c_d, 0, "c_raw0", 2)
        aw_t = wraw.tile([P, 4 * M], BF16, name="aw_t", tag="act", bufs=4)
        nc.sync.dma_start(out=aw_t[:].rearrange("p (i k) -> p i k", i=2), in_=aw_d[:])
        aw_raw = aw_t[:].bitcast(F32)
        nc.sync.dma_start(out=vec[8:10, :], in_=attn_out_b.rearrange("(r c) -> r c", c=256))
        nc.sync.dma_start(out=vec[0:4, :], in_=gate_b.rearrange("(r c) -> r c", c=256))
        nc.sync.dma_start(out=vec[4:8, :], in_=op_b.rearrange("(r c) -> r c", c=256))
        load_x(0, 0, 2)
        w_raw = [load_w(0)]
        load_x(0, 1, 2)
        q_raw0 = load_512(q_d, 0, "q_raw0", 1)
        c_raw1 = load_512(c_d, 1, "c_raw1", 1)
        w_raw.append(load_w(1))
        w_raw.append(load_w(2))
        load_x(1, 0, 1)
        w_raw.append(load_w(3))
        q_raw1 = load_512(q_d, 1, "q_raw1", 1)
        nc.sync.dma_start(out=lg_bc[:], in_=ln_g.partition_broadcast(P))
        nc.sync.dma_start(out=lb_bc[:], in_=ln_b.partition_broadcast(P))

        def turn(words, base, row_words):
            tp = psum.tile([P, 2, 256], F32, name="tp", tag="bank")
            for u in range(2):
                for e in range(2):
                    o = base + e * row_words + u * P
                    nc.tensor.transpose(tp[:, u, e * P : (e + 1) * P], words[:, o : o + P], ident_f[:])
            return tp

        def lay(tp, dst_bf16, eng):
            dst = dst_bf16.bitcast(F32).rearrange("p (r u) -> p r u", u=2)
            src = tp[:].rearrange("p u r -> p r u")
            if eng == "v":
                nc.vector.tensor_copy(out=dst, in_=src)
            else:
                nc.scalar.copy(out=dst, in_=src)

        def quant(src, codes, scales):
            nc.vector.quantize_mx(out=codes.bitcast(FP8X4), scales=scales, in_=src)

        def mx(acc, lw, lsc, rw, rsc, start, stop):
            nc.tensor.matmul_mx(
                out=acc, lhsT=lw.bitcast(FP8X4), lhsT_scale=lsc, rhs=rw.bitcast(FP8X4), rhs_scale=rsc,
                start=start, stop=stop,
            )

        def turn_512(words):
            return [turn(words, il * M, M // 2) for il in range(2)]

        def lay_512(tps, eng):
            g = grp.tile([P, 4 * HALF], BF16, name="g_512", tag="ga", align_bytes=64)
            for il in range(2):
                lay(tps[il], g[:, il * 1024 : (il + 1) * 1024], eng)
            return g

        x_words = x_raw[:].rearrange("p h k -> p (h k)").bitcast(F32)

        def x_turn(i):
            return [turn(x_words, i * D + g * 256, D // 2) for g in range(2)]

        def x_lay(i, tps, engs):
            for g in range(2):
                a = ((i // 2 * 2 + g) * HALF + i % 2 * 256) * 4
                lay(tps[g], gx[:, a : a + 1024], engs[g])

        def x_quant(th, g):
            a = th * 1536 + g * 512
            quant(gx[:, (th * 2 + g) * 2048 : (th * 2 + g + 1) * 2048], gc[:, a : a + 512], gs[:, a : a + 512])

        def q_quant(th, g):
            a = th * 1536 + 1024
            quant(g[:], gc[:, a : a + 512], gs[:, a : a + 512])

        def w_turn(i):
            g_w, o_w = w_raw[i]
            return [turn(g_w, s * 256, (D + M) // 2) for s in range(3)] + [turn(o_w, 0, M // 2)]

        def w_tile():
            g_w = grp.tile([P, 4 * 4 * 256], BF16, name="g_w", tag="gw", align_bytes=64, bufs=2)
            return g_w

        def w_lay(g, tps, h, engs):
            for s in (2 * h, 2 * h + 1):
                lay(tps[s], g[:, s * 1024 : (s + 1) * 1024], engs[s])

        def w_quant(i, g, h):
            a = i * 1024 + h * 512
            quant(g[:, h * 2048 : (h + 1) * 2048], wc[:, a : a + 512], ws[:, a : a + 512])

        def mm1(th):
            banks = []
            for n in range(4):
                p1 = psum.tile([P, 4, P], F32, name="p1", tag="bank")
                c = slice(th * HALF + n * P, th * HALF + (n + 1) * P)
                for t in range(4):
                    mx(p1[:, t, :], wa[:, t * P : (t + 1) * P], was[:, t * P : (t + 1) * P], cc[:, c], cs[:, c], True, True)
                banks.append(p1)
            return banks

        def r_lay(banks):
            g_r = grp.tile([P, HALF, 4], BF16, name="g_r", tag="ga", align_bytes=64)
            for n in range(4):
                nc.vector.tensor_tensor(
                    out=g_r[:, n * P : (n + 1) * P, :], in0=banks[n][:].rearrange("p t c -> p c t"),
                    in1=ab[:].unsqueeze(1).to_broadcast([P, P, 4]), op=ALU.add,
                )
            return g_r

        def r_quant(th, g_r):
            tok = slice(th * HALF, (th + 1) * HALF)
            quant(g_r[:].rearrange("p c t -> p (c t)"), rc[:, tok], rs[:, tok])

        def gating(th, i):
            tok = slice(th * HALF, (th + 1) * HALF)
            banks = []
            for e in range(2):
                p2 = psum.tile([P, HALF], F32, name="p2", tag="bank")
                a = (i * 4 + 3) * 256 + e * P
                mx(p2[:], wc[:, a : a + P], ws[:, a : a + P], rc[:, tok], rs[:, tok], True, True)
                p3 = psum.tile([P, HALF], F32, name="p3", tag="bank")
                for s in range(3):
                    a = (i * 4 + s) * 256 + e * P
                    b = (th * 3 + s) * HALF
                    mx(p3[:], wc[:, a : a + P], ws[:, a : a + P], gc[:, b : b + HALF], gs[:, b : b + HALF], s == 0, s == 2)
                banks.append((p2, p3))
            return banks

        def sigm(i, e, banks):
            d = 2 * i + e
            h_t = gwork.tile([P, HALF], F32, name="h_t", tag="h")
            nc.scalar.activation(out=h_t[:], in_=banks[e][1][:], func=ACT.Sigmoid, bias=ngb[:, d : d + 1], scale=-1.0)
            return h_t

        def diff(th, i, e, banks):
            d = 2 * i + e
            e_t = gwork.tile([P, HALF], F32, name="e_t", tag="e")
            nc.vector.scalar_tensor_tensor(
                out=e_t[:], in0=banks[e][0][:], scalar=ob[:, d : d + 1], in1=gx5[:, th, i // 2, :, 2 * (i % 2) + e],
                op0=ALU.add, op1=ALU.subtract,
            )
            return e_t

        def mul(th, i, e, h_t, e_t):
            late = i >= 2 if th == 0 else (i, e) == (3, 1)
            eng = nc.vector if late else nc.gpsimd
            eng.tensor_tensor(out=m_half[th][:, 2 * i + e, :], in0=h_t[:], in1=e_t[:], op=ALU.mult)

        def y_tile(k):
            th, j = k // 4, k % 4
            banks = []
            for g in range(2):
                yp = psum.tile([P, 2, 256], F32, name="yp", tag="bank")
                banks.append(yp)
                o = j * D + g * 512
                nc.tensor.matmul(
                    out=yp[:], lhsT=ident_b[:], rhs=x_raw[:, th, o : o + 512].rearrange("p (a e) -> p e a", e=2),
                    start=True, stop=False,
                )
                for e in range(2):
                    for u in range(2):
                        nc.tensor.matmul(
                            out=yp[:, e, u * P : (u + 1) * P], lhsT=m_half[th][:, 2 * (2 * g + u) + e, j * P : (j + 1) * P],
                            rhs=ident_f[:], is_transpose=True, start=False, stop=(e == 1 and u == 1),
                        )
            return banks

        def sums(banks):
            y_t = lny.tile([P, D], F32, name="y_t", tag="y", bufs=3)
            s1 = small.tile([P, 2], F32, name="s1", tag="s1")
            for g in range(2):
                nc.scalar.activation(
                    out=y_t[:, g * 512 : (g + 1) * 512], in_=banks[g][:].rearrange("p e a -> p (e a)"),
                    func=ACT.Identity, scale=-1.0 / D, accum_out=s1[:, g : g + 1],
                )
            return y_t, s1

        def minus_mean(s1):
            nmean = small.tile([P, 1], F32, name="nmean", tag="nmean")
            nc.scalar.activation(out=nmean[:], in_=s1[:, 0:1], func=ACT.Identity, bias=s1[:, 1:2], scale=1.0)
            return nmean

        def squares(y_t, nmean):
            junk = lny.tile([P, D], BF16, name="junk", tag="junk")
            s2 = small.tile([P, 1], F32, name="s2", tag="s2")
            nc.scalar.activation(
                out=junk[:], in_=y_t[:], func=ACT.Square, bias=nmean[:], scale=-1.0 * D, accum_out=s2[:]
            )
            return s2

        def rstd_of(s2):
            ve = small.tile([P, 1], F32, name="ve", tag="ve")
            nc.gpsimd.tensor_scalar(out=ve[:], in0=s2[:], scalar1=1.0 / D, scalar2=LN_EPS, op0=ALU.mult, op1=ALU.add)
            rstd = small.tile([P, 1], F32, name="rstd", tag="rstd")
            nc.gpsimd.tensor_tensor(out=rstd[:], in0=ve[:], in1=mhalf[:], op=ALU.pow)
            return rstd

        def scale(banks, nmean):
            w_t = lnw.tile([P, D], F32, name="w_t", tag="w")
            for g in range(2):
                nc.vector.scalar_tensor_tensor(
                    out=w_t[:, g * 512 : (g + 1) * 512].rearrange("p (a e) -> p a e", e=2),
                    in0=banks[g][:].rearrange("p e a -> p a e"), scalar=nmean[:],
                    in1=lg_bc[:, g * 512 : (g + 1) * 512].rearrange("p (a e) -> p a e", e=2),
                    op0=ALU.add, op1=ALU.mult,
                )
            return w_t

        def finish(k, w_t, rstd):
            pieces = 2 if k >= 6 else 1
            width = D // pieces
            for c in range(pieces):
                cols = slice(c * width, (c + 1) * width)
                nc.vector.scalar_tensor_tensor(
                    out=w_t[:, cols], in0=w_t[:, cols], scalar=rstd[:], in1=lb_bc[:, cols], op0=ALU.mult, op1=ALU.add
                )
                nc.sync.dma_start(out=out_d[:, k // 4, k % 4, cols], in_=w_t[:, cols])

        t_c0 = turn_512(c_raw0)
        t_aw = turn_512(aw_raw)
        g_c0 = lay_512(t_c0, "s")
        g_aw = lay_512(t_aw, "s")
        quant(g_c0[:], cc[:, 0:HALF], cs[:, 0:HALF])
        quant(g_aw[:], wa[:], was[:])
        t_xa = x_turn(0)
        vt = psum.tile([P, 2, 256], F32, name="vt", tag="bank")
        nc.tensor.transpose(vt[:, 0, 0:P], vec[:].bitcast(F32), ident_f[:])
        vt_b = vt[:, 0, 0:16].bitcast(BF16)
        ab = keep.tile([P, 4], F32)
        nc.vector.tensor_copy(out=ab[:], in_=vt_b[:, 16:20])
        ngb = keep.tile([P, 8], F32)
        nc.vector.tensor_scalar_mul(out=ngb[:], in0=vt_b[:, 0:8], scalar1=-1.0)
        ob = keep.tile([P, 8], F32)
        nc.vector.tensor_copy(out=ob[:], in_=vt_b[:, 8:16])
        b_r = mm1(0)
        x_lay(0, t_xa, "ss")
        g_r = r_lay(b_r)
        t_w = w_turn(0)
        g_w = w_tile()
        w_lay(g_w, t_w, 0, "ssvs")
        w_lay(g_w, t_w, 1, "ssvs")
        t_xb = x_turn(1)
        x_lay(1, t_xb, "ss")
        t_q = turn_512(q_raw0)
        g_q = lay_512(t_q, "s")
        r_quant(0, g_r)
        w_quant(0, g_w, 0)
        w_quant(0, g_w, 1)
        x_quant(0, 0)
        x_quant(0, 1)
        q_quant(0, g_q)
        t_c1 = turn_512(c_raw1)
        g_c1 = lay_512(t_c1, "s")
        quant(g_c1[:], cc[:, HALF:T], cs[:, HALF:T])
        t_w = w_turn(1)

        for i in range(4):
            if i == 3:
                t_q = turn_512(q_raw1)
                g_q = lay_512(t_q, "s")
                x_quant(1, 1)
                q_quant(1, g_q)
            banks = gating(0, i)
            if i == 0:
                b_r = mm1(1)
            if i == 1 or i == 2:
                t_x = x_turn(i + 1)
            if i < 2:
                t_next = w_turn(i + 2)
            if i < 3:
                g_w = w_tile()
            e_ts = [diff(0, i, 0, banks)]
            for h in range(2 if i < 3 else 0):
                w_lay(g_w, t_w, h, "ssss")
                w_quant(i + 1, g_w, h)
            e_ts.append(diff(0, i, 1, banks))
            for e in range(2):
                mul(0, i, e, sigm(i, e, banks), e_ts[e])
            if i < 2:
                t_w = t_next
            if i == 0:
                g_r = r_lay(b_r)
            if i == 1:
                r_quant(1, g_r)
                x_lay(2, t_x, "sv")
            if i == 2:
                x_lay(3, t_x, "ss")
                x_quant(1, 0)

        first = None
        second = None
        for n in range(10):
            if n < 4:
                banks = gating(1, n)
            if n < 8:
                ybanks = y_tile(n)
            if n < 4:
                h_ts = [sigm(n, e, banks) for e in range(2)]
            if n < 8:
                y_t, s1 = sums(ybanks)
            if first is not None:
                s2 = squares(first[2], first[3])
            if n < 8:
                nmean = minus_mean(s1)
            if n < 4:
                mul(1, n, 0, h_ts[0], diff(1, n, 0, banks))
            if first is not None:
                scaled = (first[0], scale(first[1], first[3]))
            if n < 4:
                mul(1, n, 1, h_ts[1], diff(1, n, 1, banks))
            if second is not None:
                finish(*second)
            second = scaled + (rstd_of(s2),) if first is not None else None
            first = (n, ybanks, y_t, nmean) if n < 8 else None
